import numpy as np
import ml_dtypes


def mxq(x, axis, fmt="e4m3"):
    dtype, down = {"e4m3": (ml_dtypes.float8_e4m3fn, 7), "e5m2": (ml_dtypes.float8_e5m2, 14)}[fmt]
    v = np.moveaxis(np.asarray(x, np.float32).astype(ml_dtypes.bfloat16).astype(np.float64), axis, -1)
    blocks = v.reshape(v.shape[:-1] + (-1, 32))
    amax = np.abs(blocks).max(-1, keepdims=True)
    byte = np.maximum(np.where(amax > 0, np.frexp(amax)[1] - 1 + 127, 0) - down, 1)
    scale = np.exp2(byte - 127.0)
    codes = (blocks / scale).astype(np.float32).astype(dtype).astype(np.float64)
    return np.moveaxis((codes * scale).reshape(v.shape), -1, axis)


WIDE = False


def mx_kscale(k):
    if not WIDE:
        return np.ones(k)
    levels = np.array([10, -10, 5, -5, 0])
    if k % 512:
        return np.exp2(np.random.permutation(np.resize(levels, k // 32))).repeat(32)
    a = np.empty((k // 512, 16))
    for p in range(k // 512):
        a[p, :8] = np.random.permutation(np.resize(levels, 8))
        for g in range(8):
            far = levels[np.abs(levels - a[p, g]) >= 10]
            a[p, g + 8] = far[np.random.randint(len(far))]
    return np.exp2(a.ravel()).repeat(32)


BF16 = ml_dtypes.bfloat16


def bf(x):
    return np.asarray(x, np.float32).astype(BF16)


def f64(x):
    return np.asarray(x).astype(np.float64)


B, IN, OUT = 16384, 512, 512
EPS = 1e-5


def setup_inputs():
    s = mx_kscale(IN)
    return {"x": bf(np.random.standard_normal((B, IN)) * s),
            "weight": bf(np.random.standard_normal((OUT, IN)) / np.sqrt(IN) / s[None, :]),
            "bias": bf(np.random.standard_normal(OUT) * 0.1),
            "bn_weight": bf(1.0 + 0.1 * np.random.standard_normal(OUT)),
            "bn_bias": bf(np.random.standard_normal(OUT) * 0.1),
            "bn_mean": bf(np.random.standard_normal(OUT) * 0.1),
            "bn_var": bf(np.random.uniform(0.5, 1.5, OUT)),
            "gn_weight": bf(1.0 + 0.25 * np.sqrt(OUT) * np.random.standard_normal(OUT)),
            "gn_bias": bf(0.15 + 0.1 * np.random.standard_normal(OUT))}


def reference(x, weight, bias, bn_weight, bn_bias, bn_mean, bn_var, gn_weight, gn_bias):
    y = (mxq(f64(x), 1, "e4m3") @ mxq(f64(weight), 1, "e4m3").T) + f64(bias)
    y = (y - f64(bn_mean)) / np.sqrt(f64(bn_var) + EPS) * f64(bn_weight) + f64(bn_bias)
    y = y * 0.5 * (1.0 + np.tanh(0.797885 * y + 0.035677 * y * y * y))
    mean = np.mean(y, axis=1, keepdims=True)
    var = np.mean(y * y, axis=1, keepdims=True) - mean * mean
    gn = (y - mean) / np.sqrt(var + EPS) * f64(gn_weight) + f64(gn_bias)
    out = np.maximum(np.mean(gn, axis=1, keepdims=True), 0.0)
    return out

@@ -1,0 +1,442 @@
+import math
+from contextlib import ExitStack
+
+import concourse.mybir as mybir
+from concourse.masks import make_identity
+
+F32 = mybir.dt.float32
+BF16 = mybir.dt.bfloat16
+U32 = mybir.dt.uint32
+U8 = mybir.dt.uint8
+FP8X4 = mybir.dt.float8_e4m3fn_x4
+ACT = mybir.ActivationFunctionType
+ALU = mybir.AluOpType
+AX = mybir.AxisListType
+
+P = 128
+B, IN, OUT = 16384, 512, 512
+EPS = 1e-5
+C1, C2 = 0.797885, 0.035677
+NT = B // P
+GT = 4
+GW = GT * P
+NG = NT // GT
+CHUNKS = (4, 4) + (8,) * 15
+NJ = OUT // P
+X_TWO_BANKS = 5
+LAST_GP = 28
+
+FLOPS = 2 * B * IN * OUT
+
+
+def tile_modelnew_kernel(
+    tc, x, weight, bias, bn_weight, bn_bias, bn_mean, bn_var, gn_weight, gn_bias, out
+):
+    nc = tc.nc
+    with ExitStack() as ctx:
+        ctx.enter_context(tc.manual_schedule())
+        const = ctx.enter_context(tc.tile_pool(name="const", bufs=1))
+        xin = ctx.enter_context(tc.tile_pool(name="xin", bufs=1))
+        work2 = ctx.enter_context(tc.tile_pool(name="work2", bufs=2))
+        work3 = ctx.enter_context(tc.tile_pool(name="work3", bufs=3))
+        work4 = ctx.enter_context(tc.tile_pool(name="work4", bufs=4))
+        psum = ctx.enter_context(tc.psum_pool(name="psum", bufs=1))
+
+        w_sb = const.tile([P, NJ * IN], BF16)
+        nc.sync.dma_start(
+            out=w_sb[:].rearrange("p (j k) -> p j k", k=IN),
+            in_=weight.rearrange("(j p) k -> p j k", p=P),
+        )
+        pv = const.tile([P, P], BF16)
+        nc.gpsimd.memset(pv[:], 0.0)
+        for v, vec in enumerate((bias, bn_weight, bn_bias, bn_mean, bn_var, gn_weight)):
+            nc.scalar.dma_start(
+                out=pv[NJ * v : NJ * v + NJ, :], in_=vec.rearrange("(j p) -> j p", p=P)
+            )
+        zero = const.tile([P, 1], F32)
+        nc.vector.memset(zero[:], 0.0)
+        mhalf = const.tile([P, NJ], F32)
+        nc.vector.memset(mhalf[:], -0.5)
+        eps1 = const.tile([P, 1], F32)
+        nc.vector.memset(eps1[:], EPS)
+        eps2 = const.tile([P, 1], F32)
+        nc.vector.memset(eps2[:], EPS * OUT * OUT)
+        warm0 = const.tile([P, 1], F32)
+        nc.scalar.activation(out=warm0[:], in_=zero[:], func=ACT.Sigmoid, bias=zero[:, 0:1], scale=1.0)
+        gwb = const.tile([P, OUT], BF16)
+        gbb = const.tile([P, OUT], BF16)
+
+        x_rows = x.rearrange("(p t) k -> p (t k)", t=NT)
+        x_of = []
+        t0 = 0
+        for c, n_tiles in enumerate(CHUNKS):
+            xc = xin.tile([P, n_tiles * IN], BF16, tag="x%d" % c, name="xc")
+            nc.sync.dma_start(out=xc[:], in_=x_rows[:, t0 * IN : (t0 + n_tiles) * IN])
+            for q in range(n_tiles // GT):
+                x_of.append((xc, q * GT * IN))
+            t0 += n_tiles
+            if c == 2:
+                nc.sync.dma_start(out=gwb[:], in_=gn_weight.partition_broadcast(P))
+                nc.sync.dma_start(out=gbb[:], in_=gn_bias.partition_broadcast(P))
+
+        ident = const.tile([P, P], F32)
+        make_identity(nc, ident[:])
+        ident_b = const.tile([P, P], BF16)
+        make_identity(nc, ident_b[:])
+
+        def transposes(src, col0, b, tag):
+            words = src[:].bitcast(F32)
+            xt = psum.tile([P, 2, 2, P], F32, tag=tag, name="xt_" + tag)
+            for t2 in range(2):
+                for u in range(2):
+                    w0 = col0 // 2 + (2 * b + t2) * (IN // 2)
+                    nc.tensor.transpose(
+                        xt[:, t2, u, :], words[:, w0 + u : w0 + IN // 2 : 2], ident[:]
+                    )
+            return xt
+
+        def copy_out(grouped, xt, b, engine):
+            gw32 = grouped[:].bitcast(F32)
+            dst = gw32[:, b * 512 : (b + 1) * 512].rearrange("p (t r u) -> p t r u", t=2, u=2)
+            srcv = xt[:].rearrange("p t u r -> p t r u")
+            if engine == "s":
+                nc.scalar.copy(out=dst, in_=srcv)
+            else:
+                nc.vector.tensor_copy(out=dst, in_=srcv)
+
+        wq = const.tile([P, OUT], U32, align_bytes=64)
+        ws = const.tile([P, OUT], U8, align_bytes=64)
+        pf = const.tile([P, 6 * NJ], F32)
+        a_c = const.tile([P, NJ], F32)
+        b_c = const.tile([P, NJ], F32)
+        r = math.sqrt(C2)
+        sc1 = const.tile([P, NJ], F32)
+        bi1 = const.tile([P, NJ], F32)
+        s_c = const.tile([P, NJ], F32)
+        sc2 = const.tile([P, NJ], F32)
+        bi2 = const.tile([P, NJ], F32)
+        bb = const.tile([P, NJ], F32)
+        nh_sgw = const.tile([P, 1], F32)
+        mgb = const.tile([P, 1], F32)
+
+        st = const.tile([P, NT, 6], F32)
+        traw = const.tile([P, NT], F32)
+        junk = const.tile([P, OUT], F32)
+        junk_s = const.tile([P, OUT], F32)
+
+        banks_of = {}
+        grouped_of = {}
+        xq_of = {}
+        acc_of = {}
+        c_of = {}
+        z_of = {}
+        yT_of = {}
+
+        def ok(g):
+            return 0 <= g < NG
+
+        def pe_xt(g, b):
+            if ok(g):
+                tag = "xt%d" % b if g < X_TWO_BANKS else "xt0"
+                banks_of[(g, b)] = transposes(x_of[g][0], x_of[g][1], b, tag)
+
+        def evac(g, b, engine):
+            if ok(g):
+                if b == 0:
+                    grouped_of[g] = work2.tile(
+                        [P, GW * 4], BF16, tag="grouped", name="grouped", align_bytes=64
+                    )
+                copy_out(grouped_of[g], banks_of[(g, b)], b, engine)
+
+        def quant(g):
+            if ok(g):
+                xq = work2.tile([P, GW], U32, tag="xq", align_bytes=64)
+                xs = work2.tile([P, GW], U8, tag="xs", align_bytes=64)
+                nc.vector.quantize_mx(out=xq[:].bitcast(FP8X4), scales=xs[:], in_=grouped_of[g][:])
+                xq_of[g] = (xq, xs)
+
+        def mx(g, js):
+            if ok(g):
+                xq, xs = xq_of[g]
+                for j in js:
+                    acc = psum.tile([P, GW], F32, tag="acc%d" % j, name="acc%d" % j)
+                    nc.tensor.matmul_mx(
+                        out=acc[:],
+                        lhsT=wq[:, j * P : (j + 1) * P].bitcast(FP8X4),
+                        lhsT_scale=ws[:, j * P : (j + 1) * P],
+                        rhs=xq[:].bitcast(FP8X4),
+                        rhs_scale=xs[:],
+                        start=True,
+                        stop=True,
+                    )
+                    acc_of[(g, j)] = acc
+
+        def z_on_vector(g, j):
+            return g in (0, 1) and j == 1
+
+        def s_square_z(g, js):
+            if ok(g):
+                if js[0] == 0:
+                    c_of[g] = work4.tile([P, NJ * GW], F32, tag="c", name="c")
+                    z_of[g] = work3.tile([P, NJ * GW], F32, tag="z", name="z")
+                for j in js:
+                    if not z_on_vector(g, j):
+                        nc.scalar.activation(
+                            out=z_of[g][:, j * GW : (j + 1) * GW],
+                            in_=acc_of[(g, j)][:],
+                            func=ACT.Identity,
+                            bias=b_c[:, j : j + 1],
+                            scale=a_c[:, j : j + 1],
+                        )
+                    nc.scalar.activation(
+                        out=c_of[g][:, j * GW : (j + 1) * GW],
+                        in_=acc_of[(g, j)][:],
+                        func=ACT.Square,
+                        bias=bi1[:, j : j + 1],
+                        scale=sc1[:, j : j + 1],
+                    )
+
+        def v_cubic(g, js):
+            if ok(g):
+                for j in js:
+                    cj = c_of[g][:, j * GW : (j + 1) * GW]
+                    nc.vector.scalar_tensor_tensor(
+                        out=cj,
+                        in0=cj,
+                        scalar=s_c[:, j : j + 1],
+                        in1=acc_of[(g, j)][:],
+                        op0=ALU.add,
+                        op1=ALU.mult,
+                    )
+                    if z_on_vector(g, j):
+                        nc.vector.tensor_scalar(
+                            out=z_of[g][:, j * GW : (j + 1) * GW],
+                            in0=acc_of[(g, j)][:],
+                            scalar1=a_c[:, j : j + 1],
+                            scalar2=b_c[:, j : j + 1],
+                            op0=ALU.mult,
+                            op1=ALU.add,
+                        )
+
+        def s_sigmoid(g, js):
+            if ok(g):
+                for j in js:
+                    cj = c_of[g][:, j * GW : (j + 1) * GW]
+                    nc.scalar.activation(
+                        out=cj,
+                        in_=cj,
+                        func=ACT.Sigmoid,
+                        bias=bi2[:, j : j + 1],
+                        scale=sc2[:, j : j + 1],
+                    )
+
+        def g_mul(g, js):
+            if ok(g):
+                cols = slice(js[0] * GW, (js[-1] + 1) * GW)
+                nc.gpsimd.tensor_tensor(
+                    out=c_of[g][:, cols], in0=c_of[g][:, cols], in1=z_of[g][:, cols], op=ALU.mult
+                )
+
+        w_of = {}
+        w4_of = {}
+
+        def by_gpsimd(g):
+            return 0 <= g <= LAST_GP
+
+        def g_weigh(g, js):
+            if by_gpsimd(g):
+                if js[0] == 0:
+                    w_of[g] = work2.tile([P, NJ, P], F32, tag="w", name="w")
+                for j in js:
+                    nc.gpsimd.tensor_scalar(
+                        out=w_of[g][:, j, :],
+                        in0=c_of[g][:, j * GW + (GT - 1) * P : (j + 1) * GW],
+                        scalar1=pf[:, 5 * NJ + j : 5 * NJ + j + 1],
+                        scalar2=zero[:, 0:1],
+                        op0=ALU.mult,
+                        op1=ALU.add,
+                    )
+
+        def pe_wt(g):
+            if by_gpsimd(g):
+                w4 = psum.tile([P, P], F32, tag="xt1", name="w4")
+                for j in range(NJ):
+                    nc.tensor.matmul(
+                        out=w4[:],
+                        lhsT=w_of[g][:, j, :],
+                        rhs=ident[:],
+                        is_transpose=True,
+                        start=(j == 0),
+                        stop=(j == NJ - 1),
+                    )
+                w4_of[g] = w4
+
+        def v_red(g):
+            if by_gpsimd(g):
+                tt = g * GT + GT - 1
+                nc.vector.tensor_reduce(
+                    out=traw[:, tt : tt + 1], in_=w4_of[g][:], axis=AX.X, op=ALU.add
+                )
+
+        def pe_yt(g, t):
+            if ok(g):
+                yT = psum.tile([P, OUT], F32, tag="yT%d" % (t % 2), name="yT%d" % (t % 2))
+                for j in range(NJ):
+                    nc.tensor.transpose(
+                        yT[:, j * P : (j + 1) * P],
+                        c_of[g][:, j * GW + t * P : j * GW + (t + 1) * P],
+                        ident[:],
+                    )
+                yT_of[(g, t)] = yT
+
+        def v_bn(g, t):
+            if ok(g):
+                nc.vector.bn_stats(out=st[:, g * GT + t, :], in_=yT_of[(g, t)][:])
+
+        def v_dot(g, t):
+            if ok(g) and not (t == GT - 1 and by_gpsimd(g)):
+                yT = yT_of[(g, t)]
+                tt = g * GT + t
+                nc.vector.scalar_tensor_tensor(
+                    out=junk[:],
+                    in0=yT[:],
+                    scalar=1.0,
+                    in1=gwb[:],
+                    op0=ALU.mult,
+                    op1=ALU.mult,
+                    accum_out=traw[:, tt : tt + 1],
+                )
+
+        w_grouped = work2.tile([P, GW * 4], BF16, tag="grouped", align_bytes=64)
+        copy_out(w_grouped, transposes(w_sb, 0, 0, "acc0"), 0, "s")
+        copy_out(w_grouped, transposes(w_sb, 0, 1, "acc1"), 1, "s")
+        pe_xt(0, 0)
+        evac(0, 0, "s")
+        pe_xt(0, 1)
+        evac(0, 1, "s")
+        nc.vector.quantize_mx(out=wq[:].bitcast(FP8X4), scales=ws[:], in_=w_grouped[:])
+        pT = psum.tile([P, P], BF16, tag="yT0", name="pT")
+        nc.tensor.transpose(pT[:], pv[:], ident_b[:])
+        nc.vector.tensor_copy(out=pf[:], in_=pT[:, 0 : 6 * NJ])
+        nc.vector.tensor_scalar(
+            out=a_c[:], in0=pf[:, 4 * NJ : 5 * NJ], scalar1=EPS, scalar2=None, op0=ALU.add
+        )
+        nc.gpsimd.tensor_tensor(out=a_c[:], in0=a_c[:], in1=mhalf[:], op=ALU.pow)
+        nc.vector.tensor_tensor(
+            out=b_c[:], in0=pf[:, 0:NJ], in1=pf[:, 3 * NJ : 4 * NJ], op=ALU.subtract
+        )
+        pe_xt(1, 0)
+        evac(1, 0, "s")
+        pe_xt(1, 1)
+        evac(1, 1, "s")
+        quant(0)
+        nc.vector.tensor_tensor(out=a_c[:], in0=a_c[:], in1=pf[:, NJ : 2 * NJ], op=ALU.mult)
+        nc.vector.tensor_tensor(out=b_c[:], in0=b_c[:], in1=a_c[:], op=ALU.mult)
+        nc.vector.tensor_tensor(out=b_c[:], in0=b_c[:], in1=pf[:, 2 * NJ : 3 * NJ], op=ALU.add)
+        nc.vector.tensor_scalar(out=sc1[:], in0=a_c[:], scalar1=r, scalar2=None, op0=ALU.mult)
+        nc.vector.tensor_scalar(out=bi1[:], in0=b_c[:], scalar1=1.5 * r, scalar2=None, op0=ALU.mult)
+        nc.vector.tensor_tensor(out=bb[:], in0=b_c[:], in1=b_c[:], op=ALU.mult)
+        nc.vector.tensor_scalar(
+            out=s_c[:], in0=bb[:], scalar1=0.75 * C2, scalar2=C1, op0=ALU.mult, op1=ALU.add
+        )
+        nc.vector.tensor_scalar(out=sc2[:], in0=a_c[:], scalar1=2.0, scalar2=None, op0=ALU.mult)
+        nc.vector.tensor_scalar(
+            out=bb[:], in0=bb[:], scalar1=2.0 * C2, scalar2=2.0 * C1, op0=ALU.mult, op1=ALU.add
+        )
+        nc.vector.tensor_tensor(out=bi2[:], in0=bb[:], in1=b_c[:], op=ALU.mult)
+        quant(1)
+        mx(0, (0, 1, 2, 3))
+        pe_xt(2, 0)
+        pe_xt(2, 1)
+
+        for g in (0, 1):
+            s_square_z(g, (0, 1))
+            s_sigmoid(g - 1, (2, 3))
+            g_mul(g - 1, (2, 3))
+            v_cubic(g, (0, 1))
+            evac(g + 2, 0, "v")
+            mx(g + 1, (0, 1))
+            if g == 1:
+                pe_xt(g + 3, 0)
+                pe_yt(g - 1, 0)
+                pe_yt(g - 1, 1)
+            s_square_z(g, (2, 3))
+            v_cubic(g, (2, 3))
+            evac(g + 2, 1, "v")
+            quant(g + 2)
+            mx(g + 1, (2, 3))
+            if g == 0:
+                pe_xt(g + 3, 0)
+            pe_xt(g + 3, 1)
+            s_sigmoid(g, (0, 1))
+            g_mul(g, (0, 1))
+
+        for g in range(2, NG + 2):
+            e0 = "v" if g % 2 == 1 else "s"
+            if g > 2:
+                pe_xt(g + 2, 0)
+            s_square_z(g, (0, 1))
+            v_bn(g - 2, 0)
+            v_dot(g - 2, 0)
+            v_bn(g - 2, 1)
+            v_dot(g - 2, 1)
+            evac(g + 2, 0, e0)
+            pe_yt(g - 2, 2)
+            pe_yt(g - 2, 3)
+            pe_wt(g - 3)
+            if g > 2:
+                quant(g + 1)
+            s_sigmoid(g - 1, (2, 3))
+            g_mul(g - 1, (2, 3))
+            g_weigh(g - 2, (0, 1))
+            v_cubic(g, (0, 1))
+            mx(g + 1, (0, 1))
+            if g > 2:
+                pe_xt(g + 2, 1)
+            s_square_z(g, (2, 3))
+            v_bn(g - 2, 2)
+            v_dot(g - 2, 2)
+            v_bn(g - 2, 3)
+            v_dot(g - 2, 3)
+            v_red(g - 3)
+            pe_yt(g - 1, 0)
+            pe_yt(g - 1, 1)
+            v_cubic(g, (2, 3))
+            mx(g + 1, (2, 3))
+            s_sigmoid(g, (0, 1))
+            g_mul(g, (0, 1))
+            g_weigh(g - 2, (2, 3))
+            evac(g + 2, 1, "s")
+
+        nc.scalar.activation(
+            out=junk_s[:], in_=gwb[:], func=ACT.Copy, scale=-0.5, accum_out=nh_sgw[:, 0:1]
+        )
+        nc.scalar.activation(
+            out=junk_s[:], in_=gbb[:], func=ACT.Copy, scale=1.0 / OUT, accum_out=mgb[:, 0:1]
+        )
+        warm = const.tile([P, 1], F32)
+        nc.scalar.activation(out=warm[:], in_=eps1[:], func=ACT.Sqrt, bias=eps1[:, 0:1], scale=1.0)
+
+        s = const.tile([P, NT], F32)
+        d = const.tile([P, NT], F32)
+        vs = const.tile([P, NT], F32)
+        nc.vector.tensor_tensor(out=d[:], in0=st[:, :, 1], in1=st[:, :, 4], op=ALU.subtract)
+        nc.vector.tensor_tensor(out=vs[:], in0=st[:, :, 2], in1=st[:, :, 5], op=ALU.add)
+        nc.vector.scalar_tensor_tensor(
+            out=d[:], in0=d[:], scalar=float(OUT // 4), in1=d[:], op0=ALU.mult, op1=ALU.mult
+        )
+        nc.vector.tensor_tensor(out=vs[:], in0=vs[:], in1=d[:], op=ALU.add)
+        nc.scalar.activation(
+            out=vs[:], in_=vs[:], func=ACT.Sqrt, bias=eps2[:, 0:1], scale=float(OUT)
+        )
+        nc.vector.tensor_tensor(out=s[:], in0=st[:, :, 1], in1=st[:, :, 4], op=ALU.add)
+        nc.vector.scalar_tensor_tensor(
+            out=s[:], in0=s[:], scalar=nh_sgw[:, 0:1], in1=traw[:], op0=ALU.mult, op1=ALU.add
+        )
+        nc.vector.reciprocal(out=vs[:], in_=vs[:])
+        nc.vector.tensor_tensor(out=s[:], in0=s[:], in1=vs[:], op=ALU.mult)
+        res = const.tile([P, NT], F32)
+        nc.vector.tensor_scalar(
+            out=res[:], in0=s[:], scalar1=mgb[:, 0:1], scalar2=0.0, op0=ALU.add, op1=ALU.max
+        )
+        nc.sync.dma_start(out=out.rearrange("(p t) o -> p (t o)", t=NT), in_=res[:])

@@ -18,13 +18,15 @@ B, IN, OUT = 16384, 512, 512
 EPS = 1e-5
 C1, C2 = 0.797885, 0.035677
 NT = B // P
-GT = 4
-GW = GT * P
-NG = NT // GT
-CHUNKS = (4, 4) + (8,) * 15
+HW = 512
+HT = HW // P
+BW = 2 * HW
+BT = BW // P
+NB = NT // BT
 NJ = OUT // P
-X_TWO_BANKS = 5
-LAST_GP = 28
+NQ = 2 * NB
+XBUFS = 8
+TINY = 1e-30
 
 FLOPS = 2 * B * IN * OUT
 
@@ -36,10 +38,9 @@ def tile_modelnew_kernel(
     with ExitStack() as ctx:
         ctx.enter_context(tc.manual_schedule())
         const = ctx.enter_context(tc.tile_pool(name="const", bufs=1))
-        xin = ctx.enter_context(tc.tile_pool(name="xin", bufs=1))
+        xin = ctx.enter_context(tc.tile_pool(name="xin", bufs=XBUFS))
         work2 = ctx.enter_context(tc.tile_pool(name="work2", bufs=2))
         work3 = ctx.enter_context(tc.tile_pool(name="work3", bufs=3))
-        work4 = ctx.enter_context(tc.tile_pool(name="work4", bufs=4))
         psum = ctx.enter_context(tc.psum_pool(name="psum", bufs=1))
 
         w_sb = const.tile([P, NJ * IN], BF16)
@@ -67,17 +68,24 @@ def tile_modelnew_kernel(
         gbb = const.tile([P, OUT], BF16)
 
         x_rows = x.rearrange("(p t) k -> p (t k)", t=NT)
-        x_of = []
-        t0 = 0
-        for c, n_tiles in enumerate(CHUNKS):
-            xc = xin.tile([P, n_tiles * IN], BF16, tag="x%d" % c, name="xc")
-            nc.sync.dma_start(out=xc[:], in_=x_rows[:, t0 * IN : (t0 + n_tiles) * IN])
-            for q in range(n_tiles // GT):
-                x_of.append((xc, q * GT * IN))
-            t0 += n_tiles
-            if c == 2:
+        x_of = {}
+
+        def load_block(s):
+            if s < NB:
+                xc = xin.tile([P, BT * IN], BF16, tag="x", name="xc")
+                n = HT * IN if s == 0 else BT * IN
+                for c0 in range(0, BT * IN, n):
+                    nc.sync.dma_start(
+                        out=xc[:, c0 : c0 + n],
+                        in_=x_rows[:, s * BT * IN + c0 : s * BT * IN + c0 + n],
+                    )
+                x_of[s] = xc
+            if s == 2:
                 nc.sync.dma_start(out=gwb[:], in_=gn_weight.partition_broadcast(P))
                 nc.sync.dma_start(out=gbb[:], in_=gn_bias.partition_broadcast(P))
+
+        for s in range(XBUFS):
+            load_block(s)
 
         ident = const.tile([P, P], F32)
         make_identity(nc, ident[:])
@@ -109,6 +117,10 @@ def tile_modelnew_kernel(
         pf = const.tile([P, 6 * NJ], F32)
         a_c = const.tile([P, NJ], F32)
         b_c = const.tile([P, NJ], F32)
+        d_c = const.tile([P, NJ], F32)
+        be_c = const.tile([P, NJ], F32)
+        wa_c = const.tile([P, NJ], F32)
+        tmp = const.tile([P, NJ], F32)
         r = math.sqrt(C2)
         sc1 = const.tile([P, NJ], F32)
         bi1 = const.tile([P, NJ], F32)
@@ -121,7 +133,6 @@ def tile_modelnew_kernel(
 
         st = const.tile([P, NT, 6], F32)
         traw = const.tile([P, NT], F32)
-        junk = const.tile([P, OUT], F32)
         junk_s = const.tile([P, OUT], F32)
 
         banks_of = {}
@@ -130,193 +141,207 @@ def tile_modelnew_kernel(
         acc_of = {}
         c_of = {}
         z_of = {}
-        yT_of = {}
-
-        def ok(g):
-            return 0 <= g < NG
-
-        def pe_xt(g, b):
-            if ok(g):
-                tag = "xt%d" % b if g < X_TWO_BANKS else "xt0"
-                banks_of[(g, b)] = transposes(x_of[g][0], x_of[g][1], b, tag)
-
-        def evac(g, b, engine):
-            if ok(g):
-                if b == 0:
-                    grouped_of[g] = work2.tile(
-                        [P, GW * 4], BF16, tag="grouped", name="grouped", align_bytes=64
-                    )
-                copy_out(grouped_of[g], banks_of[(g, b)], b, engine)
-
-        def quant(g):
-            if ok(g):
-                xq = work2.tile([P, GW], U32, tag="xq", align_bytes=64)
-                xs = work2.tile([P, GW], U8, tag="xs", align_bytes=64)
-                nc.vector.quantize_mx(out=xq[:].bitcast(FP8X4), scales=xs[:], in_=grouped_of[g][:])
-                xq_of[g] = (xq, xs)
-
-        def mx(g, js):
-            if ok(g):
-                xq, xs = xq_of[g]
-                for j in js:
-                    acc = psum.tile([P, GW], F32, tag="acc%d" % j, name="acc%d" % j)
-                    nc.tensor.matmul_mx(
-                        out=acc[:],
-                        lhsT=wq[:, j * P : (j + 1) * P].bitcast(FP8X4),
-                        lhsT_scale=ws[:, j * P : (j + 1) * P],
-                        rhs=xq[:].bitcast(FP8X4),
-                        rhs_scale=xs[:],
-                        start=True,
-                        stop=True,
-                    )
-                    acc_of[(g, j)] = acc
-
-        def z_on_vector(g, j):
-            return g in (0, 1) and j == 1
-
-        def s_square_z(g, js):
-            if ok(g):
-                if js[0] == 0:
-                    c_of[g] = work4.tile([P, NJ * GW], F32, tag="c", name="c")
-                    z_of[g] = work3.tile([P, NJ * GW], F32, tag="z", name="z")
-                for j in js:
-                    if not z_on_vector(g, j):
-                        nc.scalar.activation(
-                            out=z_of[g][:, j * GW : (j + 1) * GW],
-                            in_=acc_of[(g, j)][:],
-                            func=ACT.Identity,
-                            bias=b_c[:, j : j + 1],
-                            scale=a_c[:, j : j + 1],
-                        )
-                    nc.scalar.activation(
-                        out=c_of[g][:, j * GW : (j + 1) * GW],
-                        in_=acc_of[(g, j)][:],
-                        func=ACT.Square,
-                        bias=bi1[:, j : j + 1],
-                        scale=sc1[:, j : j + 1],
-                    )
-
-        def v_cubic(g, js):
-            if ok(g):
-                for j in js:
-                    cj = c_of[g][:, j * GW : (j + 1) * GW]
-                    nc.vector.scalar_tensor_tensor(
-                        out=cj,
-                        in0=cj,
-                        scalar=s_c[:, j : j + 1],
-                        in1=acc_of[(g, j)][:],
-                        op0=ALU.add,
-                        op1=ALU.mult,
-                    )
-                    if z_on_vector(g, j):
-                        nc.vector.tensor_scalar(
-                            out=z_of[g][:, j * GW : (j + 1) * GW],
-                            in0=acc_of[(g, j)][:],
-                            scalar1=a_c[:, j : j + 1],
-                            scalar2=b_c[:, j : j + 1],
-                            op0=ALU.mult,
-                            op1=ALU.add,
-                        )
-
-        def s_sigmoid(g, js):
-            if ok(g):
-                for j in js:
-                    cj = c_of[g][:, j * GW : (j + 1) * GW]
-                    nc.scalar.activation(
-                        out=cj,
-                        in_=cj,
-                        func=ACT.Sigmoid,
-                        bias=bi2[:, j : j + 1],
-                        scale=sc2[:, j : j + 1],
-                    )
-
-        def g_mul(g, js):
-            if ok(g):
-                cols = slice(js[0] * GW, (js[-1] + 1) * GW)
-                nc.gpsimd.tensor_tensor(
-                    out=c_of[g][:, cols], in0=c_of[g][:, cols], in1=z_of[g][:, cols], op=ALU.mult
-                )
-
         w_of = {}
         w4_of = {}
+        yT_of = {}
 
-        def by_gpsimd(g):
-            return 0 <= g <= LAST_GP
+        def okb(s):
+            return 0 <= s < NB
 
-        def g_weigh(g, js):
-            if by_gpsimd(g):
-                if js[0] == 0:
-                    w_of[g] = work2.tile([P, NJ, P], F32, tag="w", name="w")
-                for j in js:
-                    nc.gpsimd.tensor_scalar(
-                        out=w_of[g][:, j, :],
-                        in0=c_of[g][:, j * GW + (GT - 1) * P : (j + 1) * GW],
-                        scalar1=pf[:, 5 * NJ + j : 5 * NJ + j + 1],
-                        scalar2=zero[:, 0:1],
-                        op0=ALU.mult,
-                        op1=ALU.add,
+        def okq(q):
+            return 0 <= q < NQ
+
+        def units(q, kind):
+            if not okq(q):
+                return []
+            j0 = 0 if kind == "a" else 1
+            if q // 2 in (0, NB - 1):
+                return [(j0, q % 2), (j0 + 2, q % 2)]
+            return [(j0 + 2 * (q % 2), 0), (j0 + 2 * (q % 2), 1)]
+
+        def runs(q, kind):
+            us = units(q, kind)
+            if us and us[0][0] == us[1][0]:
+                return [(us[0][0], 0, BW)]
+            return [(j, h * HW, HW) for j, h in us]
+
+        def c_at(q, j, c0, n):
+            return c_of[q // 2][:, j, c0 : c0 + n]
+
+        def pe_xt(n, tag="xt"):
+            if okb(n // 4):
+                banks_of[n] = transposes(x_of[n // 4], (n % 4) * 2 * IN, 0, tag)
+
+        def evac(n, engine="s"):
+            if okb(n // 4):
+                if n % 4 == 0:
+                    grouped_of[n // 4] = work2.tile(
+                        [P, BW * 4], BF16, tag="grouped", name="grouped", align_bytes=64
                     )
+                copy_out(grouped_of[n // 4], banks_of[n], n % 4, engine)
 
-        def pe_wt(g):
-            if by_gpsimd(g):
-                w4 = psum.tile([P, P], F32, tag="xt1", name="w4")
-                for j in range(NJ):
-                    nc.tensor.matmul(
-                        out=w4[:],
-                        lhsT=w_of[g][:, j, :],
-                        rhs=ident[:],
-                        is_transpose=True,
-                        start=(j == 0),
-                        stop=(j == NJ - 1),
-                    )
-                w4_of[g] = w4
-
-        def v_red(g):
-            if by_gpsimd(g):
-                tt = g * GT + GT - 1
-                nc.vector.tensor_reduce(
-                    out=traw[:, tt : tt + 1], in_=w4_of[g][:], axis=AX.X, op=ALU.add
+        def quant(s, c0=0, n=BW):
+            if okb(s):
+                if c0 == 0:
+                    xq = work2.tile([P, BW], U32, tag="xq", align_bytes=64)
+                    xs = work2.tile([P, BW], U8, tag="xs", align_bytes=64)
+                    xq_of[s] = (xq, xs)
+                xq, xs = xq_of[s]
+                nc.vector.quantize_mx(
+                    out=xq[:, c0 : c0 + n].bitcast(FP8X4),
+                    scales=xs[:, c0 : c0 + n],
+                    in_=grouped_of[s][:, 4 * c0 : 4 * (c0 + n)],
                 )
 
-        def pe_yt(g, t):
-            if ok(g):
-                yT = psum.tile([P, OUT], F32, tag="yT%d" % (t % 2), name="yT%d" % (t % 2))
+        def mx(q, kind, i):
+            for j, h in units(q, kind)[i : i + 1]:
+                xq, xs = xq_of[q // 2]
+                tag = "%s%d" % (kind, i)
+                acc = psum.tile([P, HW], F32, tag=tag, name="acc_" + tag)
+                cols = slice(h * HW, (h + 1) * HW)
+                nc.tensor.matmul_mx(
+                    out=acc[:],
+                    lhsT=wq[:, j * P : (j + 1) * P].bitcast(FP8X4),
+                    lhsT_scale=ws[:, j * P : (j + 1) * P],
+                    rhs=xq[:, cols].bitcast(FP8X4),
+                    rhs_scale=xs[:, cols],
+                    start=True,
+                    stop=True,
+                )
+                acc_of[(q, kind, i)] = acc
+
+        def s_z(q, i):
+            for j, h in units(q, "a")[i : i + 1]:
+                if i == 0:
+                    z_of[q] = work2.tile([P, BW], F32, tag="z", name="z")
+                nc.scalar.activation(
+                    out=z_of[q][:, i * HW : (i + 1) * HW],
+                    in_=acc_of[(q, "a", i)][:],
+                    func=ACT.Identity,
+                    bias=b_c[:, j : j + 1],
+                    scale=a_c[:, j : j + 1],
+                )
+
+        def s_sq(q, kind, i):
+            for j, h in units(q, kind)[i : i + 1]:
+                if q // 2 not in c_of:
+                    c_of[q // 2] = work3.tile([P, NJ, BW], F32, tag="c", name="c")
+                nc.scalar.activation(
+                    out=c_at(q, j, h * HW, HW),
+                    in_=acc_of[(q, kind, i)][:],
+                    func=ACT.Square,
+                    bias=bi1[:, j : j + 1],
+                    scale=sc1[:, j : j + 1],
+                )
+
+        def v_cubic(q, kind, i):
+            for j, h in units(q, kind)[i : i + 1]:
+                cj = c_at(q, j, h * HW, HW)
+                nc.vector.scalar_tensor_tensor(
+                    out=cj,
+                    in0=cj,
+                    scalar=s_c[:, j : j + 1],
+                    in1=acc_of[(q, kind, i)][:],
+                    op0=ALU.add,
+                    op1=ALU.mult,
+                )
+
+        def s_sig(q, kind, i=None):
+            parts = runs(q, kind) if i is None else [(j, h * HW, HW) for j, h in units(q, kind)[i : i + 1]]
+            for j, c0, n in parts:
+                cj = c_at(q, j, c0, n)
+                nc.scalar.activation(
+                    out=cj,
+                    in_=cj,
+                    func=ACT.Sigmoid,
+                    bias=bi2[:, j : j + 1],
+                    scale=sc2[:, j : j + 1],
+                )
+
+        def v_yhat(q, i):
+            for j, h in units(q, "v")[i : i + 1]:
+                cj = c_at(q, j, h * HW, HW)
+                nc.vector.scalar_tensor_tensor(
+                    out=cj,
+                    in0=acc_of[(q, "v", i)][:],
+                    scalar=be_c[:, j : j + 1],
+                    in1=cj,
+                    op0=ALU.add,
+                    op1=ALU.mult,
+                )
+
+        def g_mul(q):
+            z0 = 0
+            for j, c0, n in runs(q, "a"):
+                cj = c_at(q, j, c0, n)
+                nc.gpsimd.tensor_tensor(out=cj, in0=cj, in1=z_of[q][:, z0 : z0 + n], op=ALU.mult)
+                z0 += n
+
+        def product(dst, src, factor, engine):
+            if engine == "g":
+                nc.gpsimd.tensor_scalar(
+                    out=dst, in0=src, scalar1=factor, scalar2=zero[:, 0:1], op0=ALU.mult, op1=ALU.add
+                )
+            else:
+                nc.scalar.activation(out=dst, in_=src, func=ACT.Copy, scale=factor)
+
+        def weigh(q, kind, engine="g"):
+            for j, c0, n in runs(q, kind):
+                s = q // 2
+                if s not in w_of:
+                    w_of[s] = work2.tile([P, NJ, BW], F32, tag="w", name="w")
+                factor = pf[:, 5 * NJ + j : 5 * NJ + j + 1] if kind == "a" else wa_c[:, j : j + 1]
+                product(w_of[s][:, j, c0 : c0 + n], c_at(q, j, c0, n), factor, engine)
+
+        def scale(q, engine="g"):
+            for j, c0, n in runs(q, "v"):
+                product(c_at(q, j, c0, n), c_at(q, j, c0, n), d_c[:, j : j + 1], engine)
+
+        def pe_wt(p):
+            if okq(p):
+                w4 = psum.tile([P, 4, P], F32, tag="w4", name="w4")
+                for i in range(4):
+                    t = 4 * (p % 2) + i
+                    for j in range(NJ):
+                        nc.tensor.matmul(
+                            out=w4[:, i, :],
+                            lhsT=w_of[p // 2][:, j, t * P : (t + 1) * P],
+                            rhs=ident[:],
+                            is_transpose=True,
+                            start=(j == 0),
+                            stop=(j == NJ - 1),
+                        )
+                w4_of[p] = w4
+
+        def v_red(p):
+            if okq(p):
+                nc.vector.tensor_reduce(
+                    out=traw[:, 4 * p : 4 * p + 4], in_=w4_of[p][:], axis=AX.X, op=ALU.add
+                )
+
+        def pe_yt(p, i):
+            if okq(p):
+                yT = psum.tile([P, OUT], F32, tag="yT%d" % (i % 2), name="yT%d" % (i % 2))
+                t = 4 * (p % 2) + i
                 for j in range(NJ):
                     nc.tensor.transpose(
-                        yT[:, j * P : (j + 1) * P],
-                        c_of[g][:, j * GW + t * P : j * GW + (t + 1) * P],
-                        ident[:],
+                        yT[:, j * P : (j + 1) * P], c_of[p // 2][:, j, t * P : (t + 1) * P], ident[:]
                     )
-                yT_of[(g, t)] = yT
+                yT_of[(p, i)] = yT
 
-        def v_bn(g, t):
-            if ok(g):
-                nc.vector.bn_stats(out=st[:, g * GT + t, :], in_=yT_of[(g, t)][:])
+        def v_bn(p, i):
+            if okq(p):
+                nc.vector.bn_stats(out=st[:, 4 * p + i, :], in_=yT_of[(p, i)][:])
 
-        def v_dot(g, t):
-            if ok(g) and not (t == GT - 1 and by_gpsimd(g)):
-                yT = yT_of[(g, t)]
-                tt = g * GT + t
-                nc.vector.scalar_tensor_tensor(
-                    out=junk[:],
-                    in0=yT[:],
-                    scalar=1.0,
-                    in1=gwb[:],
-                    op0=ALU.mult,
-                    op1=ALU.mult,
-                    accum_out=traw[:, tt : tt + 1],
-                )
-
-        w_grouped = work2.tile([P, GW * 4], BF16, tag="grouped", align_bytes=64)
-        copy_out(w_grouped, transposes(w_sb, 0, 0, "acc0"), 0, "s")
-        copy_out(w_grouped, transposes(w_sb, 0, 1, "acc1"), 1, "s")
-        pe_xt(0, 0)
-        evac(0, 0, "s")
-        pe_xt(0, 1)
-        evac(0, 1, "s")
-        nc.vector.quantize_mx(out=wq[:].bitcast(FP8X4), scales=ws[:], in_=w_grouped[:])
+        w_grouped = const.tile([P, OUT * 4], BF16, align_bytes=64)
+        copy_out(w_grouped, transposes(w_sb, 0, 0, "a0"), 0, "s")
+        copy_out(w_grouped, transposes(w_sb, 0, 1, "a1"), 1, "s")
         pT = psum.tile([P, P], BF16, tag="yT0", name="pT")
         nc.tensor.transpose(pT[:], pv[:], ident_b[:])
+        pe_xt(0, "v0")
+        pe_xt(1, "v1")
+        pe_xt(2, "w4")
+        pe_xt(3, "yT1")
         nc.vector.tensor_copy(out=pf[:], in_=pT[:, 0 : 6 * NJ])
         nc.vector.tensor_scalar(
             out=a_c[:], in0=pf[:, 4 * NJ : 5 * NJ], scalar1=EPS, scalar2=None, op0=ALU.add
@@ -325,88 +350,113 @@ def tile_modelnew_kernel(
         nc.vector.tensor_tensor(
             out=b_c[:], in0=pf[:, 0:NJ], in1=pf[:, 3 * NJ : 4 * NJ], op=ALU.subtract
         )
-        pe_xt(1, 0)
-        evac(1, 0, "s")
-        pe_xt(1, 1)
-        evac(1, 1, "s")
-        quant(0)
+        evac(0, "s")
+        nc.vector.quantize_mx(out=wq[:].bitcast(FP8X4), scales=ws[:], in_=w_grouped[:])
         nc.vector.tensor_tensor(out=a_c[:], in0=a_c[:], in1=pf[:, NJ : 2 * NJ], op=ALU.mult)
+        evac(1, "v")
         nc.vector.tensor_tensor(out=b_c[:], in0=b_c[:], in1=a_c[:], op=ALU.mult)
-        nc.vector.tensor_tensor(out=b_c[:], in0=b_c[:], in1=pf[:, 2 * NJ : 3 * NJ], op=ALU.add)
         nc.vector.tensor_scalar(out=sc1[:], in0=a_c[:], scalar1=r, scalar2=None, op0=ALU.mult)
+        quant(0, 0, HW)
+        mx(0, "a", 0)
+        mx(0, "a", 1)
+        nc.vector.tensor_tensor(out=b_c[:], in0=b_c[:], in1=pf[:, 2 * NJ : 3 * NJ], op=ALU.add)
+        nc.vector.tensor_scalar(out=sc2[:], in0=a_c[:], scalar1=2.0, scalar2=None, op0=ALU.mult)
         nc.vector.tensor_scalar(out=bi1[:], in0=b_c[:], scalar1=1.5 * r, scalar2=None, op0=ALU.mult)
         nc.vector.tensor_tensor(out=bb[:], in0=b_c[:], in1=b_c[:], op=ALU.mult)
+        evac(2, "v")
         nc.vector.tensor_scalar(
             out=s_c[:], in0=bb[:], scalar1=0.75 * C2, scalar2=C1, op0=ALU.mult, op1=ALU.add
         )
-        nc.vector.tensor_scalar(out=sc2[:], in0=a_c[:], scalar1=2.0, scalar2=None, op0=ALU.mult)
         nc.vector.tensor_scalar(
             out=bb[:], in0=bb[:], scalar1=2.0 * C2, scalar2=2.0 * C1, op0=ALU.mult, op1=ALU.add
         )
+
         nc.vector.tensor_tensor(out=bi2[:], in0=bb[:], in1=b_c[:], op=ALU.mult)
-        quant(1)
-        mx(0, (0, 1, 2, 3))
-        pe_xt(2, 0)
-        pe_xt(2, 1)
+        nc.vector.tensor_scalar(out=tmp[:], in0=a_c[:], scalar1=-1.0, scalar2=None, op0=ALU.mult)
+        nc.vector.tensor_tensor(out=tmp[:], in0=tmp[:], in1=a_c[:], op=ALU.max)
+        nc.vector.tensor_scalar(
+            out=tmp[:], in0=tmp[:], scalar1=TINY, scalar2=2.0 * TINY, op0=ALU.is_lt, op1=ALU.mult
+        )
+        nc.vector.tensor_tensor(out=d_c[:], in0=a_c[:], in1=tmp[:], op=ALU.add)
+        nc.vector.reciprocal(out=be_c[:], in_=d_c[:])
+        nc.vector.tensor_tensor(out=be_c[:], in0=be_c[:], in1=b_c[:], op=ALU.mult)
+        nc.vector.tensor_tensor(out=wa_c[:], in0=d_c[:], in1=pf[:, 5 * NJ : 6 * NJ], op=ALU.mult)
 
-        for g in (0, 1):
-            s_square_z(g, (0, 1))
-            s_sigmoid(g - 1, (2, 3))
-            g_mul(g - 1, (2, 3))
-            v_cubic(g, (0, 1))
-            evac(g + 2, 0, "v")
-            mx(g + 1, (0, 1))
-            if g == 1:
-                pe_xt(g + 3, 0)
-                pe_yt(g - 1, 0)
-                pe_yt(g - 1, 1)
-            s_square_z(g, (2, 3))
-            v_cubic(g, (2, 3))
-            evac(g + 2, 1, "v")
-            quant(g + 2)
-            mx(g + 1, (2, 3))
-            if g == 0:
-                pe_xt(g + 3, 0)
-            pe_xt(g + 3, 1)
-            s_sigmoid(g, (0, 1))
-            g_mul(g, (0, 1))
-
-        for g in range(2, NG + 2):
-            e0 = "v" if g % 2 == 1 else "s"
-            if g > 2:
-                pe_xt(g + 2, 0)
-            s_square_z(g, (0, 1))
-            v_bn(g - 2, 0)
-            v_dot(g - 2, 0)
-            v_bn(g - 2, 1)
-            v_dot(g - 2, 1)
-            evac(g + 2, 0, e0)
-            pe_yt(g - 2, 2)
-            pe_yt(g - 2, 3)
-            pe_wt(g - 3)
-            if g > 2:
-                quant(g + 1)
-            s_sigmoid(g - 1, (2, 3))
-            g_mul(g - 1, (2, 3))
-            g_weigh(g - 2, (0, 1))
-            v_cubic(g, (0, 1))
-            mx(g + 1, (0, 1))
-            if g > 2:
-                pe_xt(g + 2, 1)
-            s_square_z(g, (2, 3))
-            v_bn(g - 2, 2)
-            v_dot(g - 2, 2)
-            v_bn(g - 2, 3)
-            v_dot(g - 2, 3)
-            v_red(g - 3)
-            pe_yt(g - 1, 0)
-            pe_yt(g - 1, 1)
-            v_cubic(g, (2, 3))
-            mx(g + 1, (2, 3))
-            s_sigmoid(g, (0, 1))
-            g_mul(g, (0, 1))
-            g_weigh(g - 2, (2, 3))
-            evac(g + 2, 1, "s")
+        for q in range(NQ + 3):
+            s, pp = q // 2, q % 2
+            rows = q - 3
+            if pp == 0 and s > 0:
+                load_block(s + XBUFS - 1)
+            v_yhat(q - 1, 0)
+            v_yhat(q - 1, 1)
+            s_z(q, 0)
+            s_sq(q, "a", 0)
+            s_z(q, 1)
+            s_sq(q, "a", 1)
+            weigh(q - 1, "v")
+            weigh(q - 1, "a")
+            scale(q - 1)
+            mx(q, "v", 0)
+            mx(q, "v", 1)
+            pe_wt(rows)
+            v_cubic(q, "a", 0)
+            v_bn(rows, 0)
+            v_cubic(q, "a", 1)
+            if q == 0:
+                evac(3, "v")
+                quant(0, HW, HW)
+                pe_xt(4)
+                pe_xt(5, "w4")
+            elif q == 1:
+                evac(6, "s")
+                evac(7, "v")
+                quant(1)
+                pe_xt(8)
+                pe_xt(9, "w4")
+                pe_xt(10, "yT0")
+                pe_xt(11, "yT1")
+            elif q == 2:
+                evac(10, "v")
+                evac(11, "v")
+                quant(2)
+            else:
+                evac(2 * q + 7)
+                pe_xt(2 * q + 8)
+            v_bn(rows, 1)
+            v_red(rows)
+            pe_yt(rows, 2)
+            pe_yt(rows, 3)
+            s_sq(q, "v", 0)
+            s_sq(q, "v", 1)
+            mx(q + 1, "a", 0)
+            mx(q + 1, "a", 1)
+            v_cubic(q, "v", 0)
+            v_cubic(q, "v", 1)
+            if pp == 0 and q > 2:
+                quant(s + 1)
+            s_sig(q, "a")
+            g_mul(q)
+            if q == 0:
+                evac(4, "s")
+                pe_xt(6)
+                evac(5, "v")
+                pe_xt(7, "w4")
+            elif q == 1:
+                evac(8, "s")
+                pe_xt(12)
+                evac(9, "v")
+            elif q == 2:
+                evac(12, "s")
+                pe_xt(13)
+            else:
+                evac(2 * q + 8)
+                pe_xt(2 * q + 9)
+            v_bn(rows, 2)
+            v_bn(rows, 3)
+            s_sig(q, "v", 0)
+            s_sig(q, "v", 1)
+            pe_yt(rows + 1, 0)
+            pe_yt(rows + 1, 1)
 
         nc.scalar.activation(
             out=junk_s[:], in_=gwb[:], func=ACT.Copy, scale=-0.5, accum_out=nh_sgw[:, 0:1]

@@ -26,7 +26,7 @@ NB = NT // BT
 NJ = OUT // P
 NQ = 2 * NB
 XBUFS = 8
-TINY = 1e-30
+TINY = 1e-18
 
 FLOPS = 2 * B * IN * OUT
 
@@ -134,6 +134,7 @@ def tile_modelnew_kernel(
         st = const.tile([P, NT, 6], F32)
         traw = const.tile([P, NT], F32)
         junk_s = const.tile([P, OUT], F32)
+        junk_r = const.tile([P, OUT], F32)
 
         banks_of = {}
         grouped_of = {}
@@ -313,15 +314,24 @@ def tile_modelnew_kernel(
                         )
                 w4_of[p] = w4
 
-        def v_red(p):
-            if okq(p):
+        def row_red(p, engine="v"):
+            if okq(p) and engine == "s":
+                for i in range(4):
+                    nc.scalar.activation(
+                        out=junk_r[:, i * P : (i + 1) * P],
+                        in_=w4_of[p][:, i, :],
+                        func=ACT.Copy,
+                        accum_out=traw[:, 4 * p + i : 4 * p + i + 1],
+                    )
+            elif okq(p):
                 nc.vector.tensor_reduce(
                     out=traw[:, 4 * p : 4 * p + 4], in_=w4_of[p][:], axis=AX.X, op=ALU.add
                 )
 
-        def pe_yt(p, i):
+        def pe_yt(p, i, tag=None):
             if okq(p):
-                yT = psum.tile([P, OUT], F32, tag="yT%d" % (i % 2), name="yT%d" % (i % 2))
+                tag = tag or "yT%d" % (i % 2)
+                yT = psum.tile([P, OUT], F32, tag=tag, name="yT_" + tag)
                 t = 4 * (p % 2) + i
                 for j in range(NJ):
                     nc.tensor.transpose(
@@ -335,7 +345,7 @@ def tile_modelnew_kernel(
 
         w_grouped = const.tile([P, OUT * 4], BF16, align_bytes=64)
         copy_out(w_grouped, transposes(w_sb, 0, 0, "a0"), 0, "s")
-        copy_out(w_grouped, transposes(w_sb, 0, 1, "a1"), 1, "s")
+        w_bank1 = transposes(w_sb, 0, 1, "a1")
         pT = psum.tile([P, P], BF16, tag="yT0", name="pT")
         nc.tensor.transpose(pT[:], pv[:], ident_b[:])
         pe_xt(0, "v0")
@@ -343,6 +353,7 @@ def tile_modelnew_kernel(
         pe_xt(2, "w4")
         pe_xt(3, "yT1")
         nc.vector.tensor_copy(out=pf[:], in_=pT[:, 0 : 6 * NJ])
+        copy_out(w_grouped, w_bank1, 1, "v")
         nc.vector.tensor_scalar(
             out=a_c[:], in0=pf[:, 4 * NJ : 5 * NJ], scalar1=EPS, scalar2=None, op0=ALU.add
         )
@@ -351,9 +362,11 @@ def tile_modelnew_kernel(
             out=b_c[:], in0=pf[:, 0:NJ], in1=pf[:, 3 * NJ : 4 * NJ], op=ALU.subtract
         )
         evac(0, "s")
+        evac(1, "s")
+        evac(2, "s")
+        evac(3, "s")
         nc.vector.quantize_mx(out=wq[:].bitcast(FP8X4), scales=ws[:], in_=w_grouped[:])
         nc.vector.tensor_tensor(out=a_c[:], in0=a_c[:], in1=pf[:, NJ : 2 * NJ], op=ALU.mult)
-        evac(1, "v")
         nc.vector.tensor_tensor(out=b_c[:], in0=b_c[:], in1=a_c[:], op=ALU.mult)
         nc.vector.tensor_scalar(out=sc1[:], in0=a_c[:], scalar1=r, scalar2=None, op0=ALU.mult)
         quant(0, 0, HW)
@@ -363,7 +376,6 @@ def tile_modelnew_kernel(
         nc.vector.tensor_scalar(out=sc2[:], in0=a_c[:], scalar1=2.0, scalar2=None, op0=ALU.mult)
         nc.vector.tensor_scalar(out=bi1[:], in0=b_c[:], scalar1=1.5 * r, scalar2=None, op0=ALU.mult)
         nc.vector.tensor_tensor(out=bb[:], in0=b_c[:], in1=b_c[:], op=ALU.mult)
-        evac(2, "v")
         nc.vector.tensor_scalar(
             out=s_c[:], in0=bb[:], scalar1=0.75 * C2, scalar2=C1, op0=ALU.mult, op1=ALU.add
         )
@@ -372,17 +384,22 @@ def tile_modelnew_kernel(
         )
 
         nc.vector.tensor_tensor(out=bi2[:], in0=bb[:], in1=b_c[:], op=ALU.mult)
-        nc.vector.tensor_scalar(out=tmp[:], in0=a_c[:], scalar1=-1.0, scalar2=None, op0=ALU.mult)
-        nc.vector.tensor_tensor(out=tmp[:], in0=tmp[:], in1=a_c[:], op=ALU.max)
-        nc.vector.tensor_scalar(
-            out=tmp[:], in0=tmp[:], scalar1=TINY, scalar2=2.0 * TINY, op0=ALU.is_lt, op1=ALU.mult
+        nc.gpsimd.tensor_tensor(out=tmp[:], in0=a_c[:], in1=a_c[:], op=ALU.mult)
+        nc.gpsimd.tensor_scalar(
+            out=tmp[:], in0=tmp[:], scalar1=TINY * TINY, scalar2=2.0 * TINY, op0=ALU.is_lt, op1=ALU.mult
         )
-        nc.vector.tensor_tensor(out=d_c[:], in0=a_c[:], in1=tmp[:], op=ALU.add)
+        nc.gpsimd.tensor_tensor(out=d_c[:], in0=a_c[:], in1=tmp[:], op=ALU.add)
+        nc.gpsimd.tensor_tensor(out=wa_c[:], in0=d_c[:], in1=pf[:, 5 * NJ : 6 * NJ], op=ALU.mult)
+        quant(0, HW, HW)
         nc.vector.reciprocal(out=be_c[:], in_=d_c[:])
         nc.vector.tensor_tensor(out=be_c[:], in0=be_c[:], in1=b_c[:], op=ALU.mult)
-        nc.vector.tensor_tensor(out=wa_c[:], in0=d_c[:], in1=pf[:, 5 * NJ : 6 * NJ], op=ALU.mult)
+        mx(0, "v", 0)
+        mx(0, "v", 1)
+        pe_xt(4, "xt")
+        pe_xt(5, "yT0")
+        pe_xt(6, "w4")
 
-        for q in range(NQ + 3):
+        for q in range(NQ):
             s, pp = q // 2, q % 2
             rows = q - 3
             if pp == 0 and s > 0:
@@ -396,24 +413,25 @@ def tile_modelnew_kernel(
             weigh(q - 1, "v")
             weigh(q - 1, "a")
             scale(q - 1)
-            mx(q, "v", 0)
-            mx(q, "v", 1)
-            pe_wt(rows)
-            v_cubic(q, "a", 0)
+            if q > 0:
+                mx(q, "v", 0)
+                mx(q, "v", 1)
+            row_red(rows - 1)
             v_bn(rows, 0)
+            v_cubic(q, "a", 0)
+            v_bn(rows, 1)
+            if q == 0:
+                evac(4, "v")
+            elif q == 1:
+                evac(7, "v")
             v_cubic(q, "a", 1)
             if q == 0:
-                evac(3, "v")
-                quant(0, HW, HW)
-                pe_xt(4)
-                pe_xt(5, "w4")
+                pe_xt(7, "yT1")
+                evac(5, "v")
             elif q == 1:
-                evac(6, "s")
-                evac(7, "v")
                 quant(1)
-                pe_xt(8)
-                pe_xt(9, "w4")
-                pe_xt(10, "yT0")
+                pe_xt(9, "yT0")
+                pe_xt(10, "w4")
                 pe_xt(11, "yT1")
             elif q == 2:
                 evac(10, "v")
@@ -421,52 +439,68 @@ def tile_modelnew_kernel(
                 quant(2)
             else:
                 evac(2 * q + 7)
-                pe_xt(2 * q + 8)
-            v_bn(rows, 1)
-            v_red(rows)
             pe_yt(rows, 2)
+            if q > 2:
+                pe_xt(2 * q + 8)
             pe_yt(rows, 3)
             s_sq(q, "v", 0)
             s_sq(q, "v", 1)
             mx(q + 1, "a", 0)
             mx(q + 1, "a", 1)
+            pe_wt(rows)
             v_cubic(q, "v", 0)
             v_cubic(q, "v", 1)
-            if pp == 0 and q > 2:
-                quant(s + 1)
+            if q > 2:
+                quant((q + 3) // 2, (q + 3) % 2 * HW, HW)
             s_sig(q, "a")
             g_mul(q)
-            if q == 0:
-                evac(4, "s")
-                pe_xt(6)
-                evac(5, "v")
-                pe_xt(7, "w4")
-            elif q == 1:
-                evac(8, "s")
-                pe_xt(12)
-                evac(9, "v")
-            elif q == 2:
-                evac(12, "s")
-                pe_xt(13)
-            else:
-                evac(2 * q + 8)
-                pe_xt(2 * q + 9)
-            v_bn(rows, 2)
-            v_bn(rows, 3)
             s_sig(q, "v", 0)
             s_sig(q, "v", 1)
+            if q == 0:
+                evac(6, "v")
+                pe_xt(8, "xt")
+            elif q == 1:
+                evac(8, "v")
+                pe_xt(12, "xt")
+                evac(9, "v")
+            elif q == 2:
+                evac(12, "v")
+                pe_xt(13, "xt")
+            else:
+                evac(2 * q + 8)
+            v_bn(rows, 2)
+            v_bn(rows, 3)
             pe_yt(rows + 1, 0)
             pe_yt(rows + 1, 1)
+            if q > 2:
+                pe_xt(2 * q + 9)
 
-        nc.scalar.activation(
-            out=junk_s[:], in_=gwb[:], func=ACT.Copy, scale=-0.5, accum_out=nh_sgw[:, 0:1]
-        )
-        nc.scalar.activation(
-            out=junk_s[:], in_=gbb[:], func=ACT.Copy, scale=1.0 / OUT, accum_out=mgb[:, 0:1]
-        )
         warm = const.tile([P, 1], F32)
         nc.scalar.activation(out=warm[:], in_=eps1[:], func=ACT.Sqrt, bias=eps1[:, 0:1], scale=1.0)
-
+        row_red(NQ - 4, "s")
+        v_yhat(NQ - 1, 0)
+        v_yhat(NQ - 1, 1)
+        weigh(NQ - 1, "v", "s")
+        weigh(NQ - 1, "a")
+        scale(NQ - 1, "s")
+        spare = ("xt", "a0", "a1", "yT0", "yT1", "v0", "v1")
+        n = 0
+        for p in range(NQ - 3, NQ):
+            for i in range(4):
+                if p > NQ - 3 or i >= 2:
+                    pe_yt(p, i, spare[n % 7])
+                    n += 1
+            pe_wt(p)
+            for i in range(4):
+                v_bn(p, i)
+            row_red(p, "s")
+            if p == NQ - 3:
+                nc.scalar.activation(
+                    out=junk_s[:], in_=gwb[:], func=ACT.Copy, scale=-0.5, accum_out=nh_sgw[:, 0:1]
+                )
+                nc.scalar.activation(
+                    out=junk_s[:], in_=gbb[:], func=ACT.Copy, scale=1.0 / OUT, accum_out=mgb[:, 0:1]
+                )
         s = const.tile([P, NT], F32)
         d = const.tile([P, NT], F32)
         vs = const.tile([P, NT], F32)

@@ -43,29 +43,29 @@ def tile_modelnew_kernel(
         work3 = ctx.enter_context(tc.tile_pool(name="work3", bufs=3))
         psum = ctx.enter_context(tc.psum_pool(name="psum", bufs=1))
 
-        w_sb = const.tile([P, NJ * IN], BF16)
-        nc.sync.dma_start(
-            out=w_sb[:].rearrange("p (j k) -> p j k", k=IN),
-            in_=weight.rearrange("(j p) k -> p j k", p=P),
-        )
+        w_sb = [const.tile([P, 2 * IN], BF16, tag="w_sb%d" % i, name="w_sb") for i in range(2)]
+
+        def load_weights(i):
+            nc.sync.dma_start(
+                out=w_sb[i][:].rearrange("p (j k) -> p j k", k=IN),
+                in_=weight[2 * i * P : 2 * (i + 1) * P, :].rearrange("(j p) k -> p j k", p=P),
+            )
+
+        load_weights(0)
         pv = const.tile([P, P], BF16)
         nc.gpsimd.memset(pv[:], 0.0)
-        for v, vec in enumerate((bias, bn_weight, bn_bias, bn_mean, bn_var, gn_weight)):
+        for v, vec in enumerate((bias, bn_weight, bn_bias, bn_mean, bn_var, gn_weight, gn_bias)):
             nc.scalar.dma_start(
                 out=pv[NJ * v : NJ * v + NJ, :], in_=vec.rearrange("(j p) -> j p", p=P)
             )
         zero = const.tile([P, 1], F32)
         nc.vector.memset(zero[:], 0.0)
-        mhalf = const.tile([P, NJ], F32)
+        mhalf = const.tile([P, P], F32)
         nc.vector.memset(mhalf[:], -0.5)
-        eps1 = const.tile([P, 1], F32)
-        nc.vector.memset(eps1[:], EPS)
-        eps2 = const.tile([P, 1], F32)
-        nc.vector.memset(eps2[:], EPS * OUT * OUT)
+        ones = const.tile([P, P], F32)
+        nc.gpsimd.memset(ones[:], 1.0)
         warm0 = const.tile([P, 1], F32)
         nc.scalar.activation(out=warm0[:], in_=zero[:], func=ACT.Sigmoid, bias=zero[:, 0:1], scale=1.0)
-        gwb = const.tile([P, OUT], BF16)
-        gbb = const.tile([P, OUT], BF16)
 
         x_rows = x.rearrange("(p t) k -> p (t k)", t=NT)
         x_of = {}
@@ -79,10 +79,9 @@ def tile_modelnew_kernel(
                         out=xc[:, c0 : c0 + n],
                         in_=x_rows[:, s * BT * IN + c0 : s * BT * IN + c0 + n],
                     )
+                    if s == 0 and c0 == 0:
+                        load_weights(1)
                 x_of[s] = xc
-            if s == 2:
-                nc.sync.dma_start(out=gwb[:], in_=gn_weight.partition_broadcast(P))
-                nc.sync.dma_start(out=gbb[:], in_=gn_bias.partition_broadcast(P))
 
         for s in range(XBUFS):
             load_block(s)
@@ -114,7 +113,7 @@ def tile_modelnew_kernel(
 
         wq = const.tile([P, OUT], U32, align_bytes=64)
         ws = const.tile([P, OUT], U8, align_bytes=64)
-        pf = const.tile([P, 6 * NJ], F32)
+        pf = const.tile([P, 7 * NJ], F32)
         a_c = const.tile([P, NJ], F32)
         b_c = const.tile([P, NJ], F32)
         d_c = const.tile([P, NJ], F32)
@@ -128,12 +127,12 @@ def tile_modelnew_kernel(
         sc2 = const.tile([P, NJ], F32)
         bi2 = const.tile([P, NJ], F32)
         bb = const.tile([P, NJ], F32)
-        nh_sgw = const.tile([P, 1], F32)
+        sums = const.tile([P, 2], F32)
+        gw_c = const.tile([P, NJ], F32)
         mgb = const.tile([P, 1], F32)
 
         st = const.tile([P, NT, 6], F32)
         traw = const.tile([P, NT], F32)
-        junk_s = const.tile([P, OUT], F32)
         junk_r = const.tile([P, OUT], F32)
 
         banks_of = {}
@@ -155,10 +154,10 @@ def tile_modelnew_kernel(
         def units(q, kind):
             if not okq(q):
                 return []
-            j0 = 0 if kind == "a" else 1
+            j0 = 0 if kind == "a" else 2
             if q // 2 in (0, NB - 1):
-                return [(j0, q % 2), (j0 + 2, q % 2)]
-            return [(j0 + 2 * (q % 2), 0), (j0 + 2 * (q % 2), 1)]
+                return [(j0, q % 2), (j0 + 1, q % 2)]
+            return [(j0 + q % 2, 0), (j0 + q % 2, 1)]
 
         def runs(q, kind):
             us = units(q, kind)
@@ -291,7 +290,7 @@ def tile_modelnew_kernel(
                 s = q // 2
                 if s not in w_of:
                     w_of[s] = work2.tile([P, NJ, BW], F32, tag="w", name="w")
-                factor = pf[:, 5 * NJ + j : 5 * NJ + j + 1] if kind == "a" else wa_c[:, j : j + 1]
+                factor = gw_c[:, j : j + 1] if kind == "a" else wa_c[:, j : j + 1]
                 product(w_of[s][:, j, c0 : c0 + n], c_at(q, j, c0, n), factor, engine)
 
         def scale(q, engine="g"):
@@ -344,34 +343,53 @@ def tile_modelnew_kernel(
                 nc.vector.bn_stats(out=st[:, 4 * p + i, :], in_=yT_of[(p, i)][:])
 
         w_grouped = const.tile([P, OUT * 4], BF16, align_bytes=64)
-        copy_out(w_grouped, transposes(w_sb, 0, 0, "a0"), 0, "s")
-        w_bank1 = transposes(w_sb, 0, 1, "a1")
+        blank = const.tile([P, HW], BF16)
+        nc.vector.memset(blank[:], 0.0)
+
+        def warm_up(n, tag):
+            blank_ps = psum.tile([P, HW], F32, tag=tag, name="blank_ps")
+            for i in range(n):
+                nc.tensor.matmul(
+                    out=blank_ps[:], lhsT=blank[:, 0:P], rhs=blank[:], start=True, stop=True
+                )
+
+        warm_up(8, "w4")
+        w_bank0 = transposes(w_sb[0], 0, 0, "a0")
+        pe_xt(0, "v0")
         pT = psum.tile([P, P], BF16, tag="yT0", name="pT")
         nc.tensor.transpose(pT[:], pv[:], ident_b[:])
-        pe_xt(0, "v0")
         pe_xt(1, "v1")
-        pe_xt(2, "w4")
-        pe_xt(3, "yT1")
-        nc.vector.tensor_copy(out=pf[:], in_=pT[:, 0 : 6 * NJ])
-        copy_out(w_grouped, w_bank1, 1, "v")
+        w_bank1 = transposes(w_sb[1], 0, 0, "a1")
+
+        def quant_w(i):
+            cols = slice(2 * i * P, 2 * (i + 1) * P)
+            nc.vector.quantize_mx(
+                out=wq[:, cols].bitcast(FP8X4),
+                scales=ws[:, cols],
+                in_=w_grouped[:, 4 * cols.start : 4 * cols.stop],
+            )
+
+        copy_out(w_grouped, w_bank0, 0, "v")
+        evac(0, "s")
+        evac(1, "s")
+        quant_w(0)
+        nc.vector.tensor_copy(out=pf[:], in_=pT[:, 0 : 7 * NJ])
         nc.vector.tensor_scalar(
             out=a_c[:], in0=pf[:, 4 * NJ : 5 * NJ], scalar1=EPS, scalar2=None, op0=ALU.add
         )
-        nc.gpsimd.tensor_tensor(out=a_c[:], in0=a_c[:], in1=mhalf[:], op=ALU.pow)
+        nc.gpsimd.tensor_tensor(out=a_c[:], in0=a_c[:], in1=mhalf[:, 0:NJ], op=ALU.pow)
         nc.vector.tensor_tensor(
             out=b_c[:], in0=pf[:, 0:NJ], in1=pf[:, 3 * NJ : 4 * NJ], op=ALU.subtract
         )
-        evac(0, "s")
-        evac(1, "s")
-        evac(2, "s")
-        evac(3, "s")
-        nc.vector.quantize_mx(out=wq[:].bitcast(FP8X4), scales=ws[:], in_=w_grouped[:])
-        nc.vector.tensor_tensor(out=a_c[:], in0=a_c[:], in1=pf[:, NJ : 2 * NJ], op=ALU.mult)
-        nc.vector.tensor_tensor(out=b_c[:], in0=b_c[:], in1=a_c[:], op=ALU.mult)
-        nc.vector.tensor_scalar(out=sc1[:], in0=a_c[:], scalar1=r, scalar2=None, op0=ALU.mult)
+        copy_out(w_grouped, w_bank1, 1, "s")
         quant(0, 0, HW)
+        nc.vector.tensor_tensor(out=a_c[:], in0=a_c[:], in1=pf[:, NJ : 2 * NJ], op=ALU.mult)
         mx(0, "a", 0)
         mx(0, "a", 1)
+        pe_xt(2, "w4")
+        nc.vector.tensor_tensor(out=b_c[:], in0=b_c[:], in1=a_c[:], op=ALU.mult)
+        nc.vector.tensor_scalar(out=sc1[:], in0=a_c[:], scalar1=r, scalar2=None, op0=ALU.mult)
+        quant_w(1)
         nc.vector.tensor_tensor(out=b_c[:], in0=b_c[:], in1=pf[:, 2 * NJ : 3 * NJ], op=ALU.add)
         nc.vector.tensor_scalar(out=sc2[:], in0=a_c[:], scalar1=2.0, scalar2=None, op0=ALU.mult)
         nc.vector.tensor_scalar(out=bi1[:], in0=b_c[:], scalar1=1.5 * r, scalar2=None, op0=ALU.mult)
@@ -382,22 +400,35 @@ def tile_modelnew_kernel(
         nc.vector.tensor_scalar(
             out=bb[:], in0=bb[:], scalar1=2.0 * C2, scalar2=2.0 * C1, op0=ALU.mult, op1=ALU.add
         )
-
         nc.vector.tensor_tensor(out=bi2[:], in0=bb[:], in1=b_c[:], op=ALU.mult)
         nc.gpsimd.tensor_tensor(out=tmp[:], in0=a_c[:], in1=a_c[:], op=ALU.mult)
         nc.gpsimd.tensor_scalar(
             out=tmp[:], in0=tmp[:], scalar1=TINY * TINY, scalar2=2.0 * TINY, op0=ALU.is_lt, op1=ALU.mult
         )
         nc.gpsimd.tensor_tensor(out=d_c[:], in0=a_c[:], in1=tmp[:], op=ALU.add)
-        nc.gpsimd.tensor_tensor(out=wa_c[:], in0=d_c[:], in1=pf[:, 5 * NJ : 6 * NJ], op=ALU.mult)
-        quant(0, HW, HW)
         nc.vector.reciprocal(out=be_c[:], in_=d_c[:])
         nc.vector.tensor_tensor(out=be_c[:], in0=be_c[:], in1=b_c[:], op=ALU.mult)
         mx(0, "v", 0)
         mx(0, "v", 1)
+        pe_xt(3, "yT1")
+        sums_ps = psum.tile([P, 2 * NJ], F32, tag="yT0", name="sums_ps")
+        nc.tensor.matmul(out=sums_ps[:], lhsT=ones[:], rhs=pf[:, 5 * NJ : 7 * NJ], start=True, stop=True)
         pe_xt(4, "xt")
-        pe_xt(5, "yT0")
-        pe_xt(6, "w4")
+
+        def row_constants():
+            nc.vector.tensor_reduce(
+                out=sums[:], in_=sums_ps[:].rearrange("p (v j) -> p v j", v=2), axis=AX.X, op=ALU.add
+            )
+            nc.vector.tensor_scalar(
+                out=mgb[:], in0=sums[:, 1:2], scalar1=1.0 / OUT, scalar2=None, op0=ALU.mult
+            )
+            nc.vector.tensor_scalar(
+                out=sums[:, 0:1], in0=sums[:, 0:1], scalar1=-1.0 / OUT, scalar2=None, op0=ALU.mult
+            )
+            nc.vector.tensor_scalar(
+                out=gw_c[:], in0=pf[:, 5 * NJ : 6 * NJ], scalar1=sums[:, 0:1], scalar2=None, op0=ALU.add
+            )
+            nc.vector.tensor_tensor(out=wa_c[:], in0=d_c[:], in1=gw_c[:], op=ALU.mult)
 
         for q in range(NQ):
             s, pp = q // 2, q % 2
@@ -410,7 +441,7 @@ def tile_modelnew_kernel(
             s_sq(q, "a", 0)
             s_z(q, 1)
             s_sq(q, "a", 1)
-            weigh(q - 1, "v")
+            weigh(q - 1, "v", "s" if q in (1, 2) else "g")
             weigh(q - 1, "a")
             scale(q - 1)
             if q > 0:
@@ -421,21 +452,31 @@ def tile_modelnew_kernel(
             v_cubic(q, "a", 0)
             v_bn(rows, 1)
             if q == 0:
-                evac(4, "v")
+                evac(2, "v")
+                pe_xt(5, "w4")
             elif q == 1:
-                evac(7, "v")
+                evac(6, "v")
+                pe_xt(9, "yT1")
+            elif q == 2:
+                evac(8, "v")
+                pe_xt(12, "w4")
             v_cubic(q, "a", 1)
             if q == 0:
-                pe_xt(7, "yT1")
-                evac(5, "v")
+                evac(3, "v")
+                pe_xt(6, "yT1")
+                quant(0, HW, HW)
+                mx(1, "a", 0)
+                mx(1, "a", 1)
             elif q == 1:
+                evac(7, "s")
+                pe_xt(10, "yT0")
+                pe_xt(11, "xt")
                 quant(1)
-                pe_xt(9, "yT0")
-                pe_xt(10, "w4")
-                pe_xt(11, "yT1")
             elif q == 2:
+                evac(9, "v")
+                evac(11, "s")
+                pe_xt(13)
                 evac(10, "v")
-                evac(11, "v")
                 quant(2)
             else:
                 evac(2 * q + 7)
@@ -443,11 +484,12 @@ def tile_modelnew_kernel(
             if q > 2:
                 pe_xt(2 * q + 8)
             pe_yt(rows, 3)
+            if q > 0:
+                mx(q + 1, "a", 0)
+                mx(q + 1, "a", 1)
+            pe_wt(rows)
             s_sq(q, "v", 0)
             s_sq(q, "v", 1)
-            mx(q + 1, "a", 0)
-            mx(q + 1, "a", 1)
-            pe_wt(rows)
             v_cubic(q, "v", 0)
             v_cubic(q, "v", 1)
             if q > 2:
@@ -457,16 +499,14 @@ def tile_modelnew_kernel(
             s_sig(q, "v", 0)
             s_sig(q, "v", 1)
             if q == 0:
-                evac(6, "v")
-                pe_xt(8, "xt")
-            elif q == 1:
-                evac(8, "v")
-                pe_xt(12, "xt")
-                evac(9, "v")
+                row_constants()
+                evac(4, "v")
+                pe_xt(7, "xt")
+                evac(5, "v")
+                pe_xt(8, "w4")
             elif q == 2:
-                evac(12, "v")
-                pe_xt(13, "xt")
-            else:
+                evac(12, "s")
+            elif q > 2:
                 evac(2 * q + 8)
             v_bn(rows, 2)
             v_bn(rows, 3)
@@ -475,52 +515,40 @@ def tile_modelnew_kernel(
             if q > 2:
                 pe_xt(2 * q + 9)
 
-        warm = const.tile([P, 1], F32)
-        nc.scalar.activation(out=warm[:], in_=eps1[:], func=ACT.Sqrt, bias=eps1[:, 0:1], scale=1.0)
         row_red(NQ - 4, "s")
         v_yhat(NQ - 1, 0)
         v_yhat(NQ - 1, 1)
         weigh(NQ - 1, "v", "s")
         weigh(NQ - 1, "a")
         scale(NQ - 1, "s")
-        spare = ("xt", "a0", "a1", "yT0", "yT1", "v0", "v1")
+        spare = ("xt", "a0", "a1", "yT0", "yT1", "v0")
         n = 0
         for p in range(NQ - 3, NQ):
             for i in range(4):
                 if p > NQ - 3 or i >= 2:
-                    pe_yt(p, i, spare[n % 7])
+                    pe_yt(p, i, spare[n % len(spare)])
                     n += 1
             pe_wt(p)
             for i in range(4):
                 v_bn(p, i)
             row_red(p, "s")
-            if p == NQ - 3:
-                nc.scalar.activation(
-                    out=junk_s[:], in_=gwb[:], func=ACT.Copy, scale=-0.5, accum_out=nh_sgw[:, 0:1]
-                )
-                nc.scalar.activation(
-                    out=junk_s[:], in_=gbb[:], func=ACT.Copy, scale=1.0 / OUT, accum_out=mgb[:, 0:1]
-                )
-        s = const.tile([P, NT], F32)
+
         d = const.tile([P, NT], F32)
         vs = const.tile([P, NT], F32)
+        res = const.tile([P, NT], F32)
         nc.vector.tensor_tensor(out=d[:], in0=st[:, :, 1], in1=st[:, :, 4], op=ALU.subtract)
-        nc.vector.tensor_tensor(out=vs[:], in0=st[:, :, 2], in1=st[:, :, 5], op=ALU.add)
+        nc.vector.scalar_tensor_tensor(
+            out=vs[:], in0=st[:, :, 2], scalar=EPS * OUT, in1=st[:, :, 5], op0=ALU.add, op1=ALU.add
+        )
         nc.vector.scalar_tensor_tensor(
             out=d[:], in0=d[:], scalar=float(OUT // 4), in1=d[:], op0=ALU.mult, op1=ALU.mult
         )
         nc.vector.tensor_tensor(out=vs[:], in0=vs[:], in1=d[:], op=ALU.add)
-        nc.scalar.activation(
-            out=vs[:], in_=vs[:], func=ACT.Sqrt, bias=eps2[:, 0:1], scale=float(OUT)
-        )
-        nc.vector.tensor_tensor(out=s[:], in0=st[:, :, 1], in1=st[:, :, 4], op=ALU.add)
+        nc.gpsimd.tensor_tensor(out=vs[:], in0=vs[:], in1=mhalf[:], op=ALU.pow)
         nc.vector.scalar_tensor_tensor(
-            out=s[:], in0=s[:], scalar=nh_sgw[:, 0:1], in1=traw[:], op0=ALU.mult, op1=ALU.add
+            out=res[:], in0=traw[:], scalar=1.0 / math.sqrt(OUT), in1=vs[:], op0=ALU.mult, op1=ALU.mult
         )
-        nc.vector.reciprocal(out=vs[:], in_=vs[:])
-        nc.vector.tensor_tensor(out=s[:], in0=s[:], in1=vs[:], op=ALU.mult)
-        res = const.tile([P, NT], F32)
         nc.vector.tensor_scalar(
-            out=res[:], in0=s[:], scalar1=mgb[:, 0:1], scalar2=0.0, op0=ALU.add, op1=ALU.max
+            out=res[:], in0=res[:], scalar1=mgb[:, 0:1], scalar2=0.0, op0=ALU.add, op1=ALU.max
         )
         nc.sync.dma_start(out=out.rearrange("(p t) o -> p (t o)", t=NT), in_=res[:])

@@ -26,6 +26,7 @@ NB = NT // BT
 NJ = OUT // P
 NQ = 2 * NB
 XBUFS = 8
+KEEP = 128
 TINY = 1e-18
 
 FLOPS = 2 * B * IN * OUT
@@ -52,20 +53,25 @@ def tile_modelnew_kernel(
             )
 
         load_weights(0)
+        zero = const.tile([P, 1], F32)
+        nc.vector.memset(zero[:], 0.0)
+        warm0 = const.tile([P, 1], F32)
+        nc.scalar.activation(out=warm0[:], in_=zero[:], func=ACT.Sigmoid, bias=zero[:, 0:1], scale=1.0)
+
         pv = const.tile([P, P], BF16)
         nc.gpsimd.memset(pv[:], 0.0)
-        for v, vec in enumerate((bias, bn_weight, bn_bias, bn_mean, bn_var, gn_weight, gn_bias)):
+        for v, vec in enumerate((bias, bn_weight, bn_bias, bn_mean, bn_var)):
             nc.scalar.dma_start(
                 out=pv[NJ * v : NJ * v + NJ, :], in_=vec.rearrange("(j p) -> j p", p=P)
             )
-        zero = const.tile([P, 1], F32)
-        nc.vector.memset(zero[:], 0.0)
-        mhalf = const.tile([P, P], F32)
+        pv2 = const.tile([P, P], BF16)
+        nc.gpsimd.memset(pv2[:], 0.0)
+        mhalf = const.tile([P, NJ], F32)
         nc.vector.memset(mhalf[:], -0.5)
         ones = const.tile([P, P], F32)
         nc.gpsimd.memset(ones[:], 1.0)
-        warm0 = const.tile([P, 1], F32)
-        nc.scalar.activation(out=warm0[:], in_=zero[:], func=ACT.Sigmoid, bias=zero[:, 0:1], scale=1.0)
+        eps1 = const.tile([P, 1], F32)
+        nc.vector.memset(eps1[:], 1.0)
 
         x_rows = x.rearrange("(p t) k -> p (t k)", t=NT)
         x_of = {}
@@ -82,6 +88,11 @@ def tile_modelnew_kernel(
                     if s == 0 and c0 == 0:
                         load_weights(1)
                 x_of[s] = xc
+            if s == 0:
+                for v, vec in enumerate((gn_weight, gn_bias)):
+                    nc.sync.dma_start(
+                        out=pv2[NJ * v : NJ * v + NJ, :], in_=vec.rearrange("(j p) -> j p", p=P)
+                    )
 
         for s in range(XBUFS):
             load_block(s)
@@ -113,7 +124,8 @@ def tile_modelnew_kernel(
 
         wq = const.tile([P, OUT], U32, align_bytes=64)
         ws = const.tile([P, OUT], U8, align_bytes=64)
-        pf = const.tile([P, 7 * NJ], F32)
+        pf = const.tile([P, 5 * NJ], F32)
+        gf = const.tile([P, 2 * NJ], F32)
         a_c = const.tile([P, NJ], F32)
         b_c = const.tile([P, NJ], F32)
         d_c = const.tile([P, NJ], F32)
@@ -285,9 +297,13 @@ def tile_modelnew_kernel(
             else:
                 nc.scalar.activation(out=dst, in_=src, func=ACT.Copy, scale=factor)
 
-        def weigh(q, kind, engine="g"):
+        def weigh(q, kind, engine="g", part=None):
             for j, c0, n in runs(q, kind):
                 s = q // 2
+                if part == "most":
+                    n -= KEEP
+                elif part == "rest":
+                    c0, n = c0 + n - KEEP, KEEP
                 if s not in w_of:
                     w_of[s] = work2.tile([P, NJ, BW], F32, tag="w", name="w")
                 factor = gw_c[:, j : j + 1] if kind == "a" else wa_c[:, j : j + 1]
@@ -353,7 +369,7 @@ def tile_modelnew_kernel(
                     out=blank_ps[:], lhsT=blank[:, 0:P], rhs=blank[:], start=True, stop=True
                 )
 
-        warm_up(8, "w4")
+        warm_up(4, "w4")
         w_bank0 = transposes(w_sb[0], 0, 0, "a0")
         pe_xt(0, "v0")
         pT = psum.tile([P, P], BF16, tag="yT0", name="pT")
@@ -373,20 +389,21 @@ def tile_modelnew_kernel(
         evac(0, "s")
         evac(1, "s")
         quant_w(0)
-        nc.vector.tensor_copy(out=pf[:], in_=pT[:, 0 : 7 * NJ])
+        nc.vector.tensor_copy(out=pf[:], in_=pT[:, 0 : 5 * NJ])
         nc.vector.tensor_scalar(
             out=a_c[:], in0=pf[:, 4 * NJ : 5 * NJ], scalar1=EPS, scalar2=None, op0=ALU.add
         )
-        nc.gpsimd.tensor_tensor(out=a_c[:], in0=a_c[:], in1=mhalf[:, 0:NJ], op=ALU.pow)
+        nc.gpsimd.tensor_tensor(out=a_c[:], in0=a_c[:], in1=mhalf[:], op=ALU.pow)
         nc.vector.tensor_tensor(
             out=b_c[:], in0=pf[:, 0:NJ], in1=pf[:, 3 * NJ : 4 * NJ], op=ALU.subtract
         )
         copy_out(w_grouped, w_bank1, 1, "s")
         quant(0, 0, HW)
         nc.vector.tensor_tensor(out=a_c[:], in0=a_c[:], in1=pf[:, NJ : 2 * NJ], op=ALU.mult)
+        pe_xt(2, "w4")
+        evac(2, "s")
         mx(0, "a", 0)
         mx(0, "a", 1)
-        pe_xt(2, "w4")
         nc.vector.tensor_tensor(out=b_c[:], in0=b_c[:], in1=a_c[:], op=ALU.mult)
         nc.vector.tensor_scalar(out=sc1[:], in0=a_c[:], scalar1=r, scalar2=None, op0=ALU.mult)
         quant_w(1)
@@ -411,11 +428,16 @@ def tile_modelnew_kernel(
         mx(0, "v", 0)
         mx(0, "v", 1)
         pe_xt(3, "yT1")
-        sums_ps = psum.tile([P, 2 * NJ], F32, tag="yT0", name="sums_ps")
-        nc.tensor.matmul(out=sums_ps[:], lhsT=ones[:], rhs=pf[:, 5 * NJ : 7 * NJ], start=True, stop=True)
-        pe_xt(4, "xt")
+        gT = psum.tile([P, P], BF16, tag="yT0", name="gT")
+        nc.tensor.transpose(gT[:], pv2[:], ident_b[:])
 
-        def row_constants():
+        def row_sums():
+            nc.vector.tensor_copy(out=gf[:], in_=gT[:, 0 : 2 * NJ])
+            sums_ps = psum.tile([P, 2 * NJ], F32, tag="xt", name="sums_ps")
+            nc.tensor.matmul(out=sums_ps[:], lhsT=ones[:], rhs=gf[:], start=True, stop=True)
+            return sums_ps
+
+        def row_constants(sums_ps):
             nc.vector.tensor_reduce(
                 out=sums[:], in_=sums_ps[:].rearrange("p (v j) -> p v j", v=2), axis=AX.X, op=ALU.add
             )
@@ -426,9 +448,9 @@ def tile_modelnew_kernel(
                 out=sums[:, 0:1], in0=sums[:, 0:1], scalar1=-1.0 / OUT, scalar2=None, op0=ALU.mult
             )
             nc.vector.tensor_scalar(
-                out=gw_c[:], in0=pf[:, 5 * NJ : 6 * NJ], scalar1=sums[:, 0:1], scalar2=None, op0=ALU.add
+                out=gw_c[:], in0=gf[:, 0:NJ], scalar1=sums[:, 0:1], scalar2=None, op0=ALU.add
             )
-            nc.vector.tensor_tensor(out=wa_c[:], in0=d_c[:], in1=gw_c[:], op=ALU.mult)
+            nc.gpsimd.tensor_tensor(out=wa_c[:], in0=d_c[:], in1=gw_c[:], op=ALU.mult)
 
         for q in range(NQ):
             s, pp = q // 2, q % 2
@@ -441,8 +463,8 @@ def tile_modelnew_kernel(
             s_sq(q, "a", 0)
             s_z(q, 1)
             s_sq(q, "a", 1)
-            weigh(q - 1, "v", "s" if q in (1, 2) else "g")
-            weigh(q - 1, "a")
+            weigh(q - 1, "v")
+            weigh(q - 1, "a", "g", "most")
             scale(q - 1)
             if q > 0:
                 mx(q, "v", 0)
@@ -452,32 +474,27 @@ def tile_modelnew_kernel(
             v_cubic(q, "a", 0)
             v_bn(rows, 1)
             if q == 0:
-                evac(2, "v")
                 pe_xt(5, "w4")
-            elif q == 1:
-                evac(6, "v")
-                pe_xt(9, "yT1")
-            elif q == 2:
-                evac(8, "v")
-                pe_xt(12, "w4")
-            v_cubic(q, "a", 1)
-            if q == 0:
                 evac(3, "v")
                 pe_xt(6, "yT1")
+            elif q == 1:
+                evac(6, "s")
+                pe_xt(9, "yT1")
+            v_cubic(q, "a", 1)
+            if q == 0:
+                sums_ps = row_sums()
                 quant(0, HW, HW)
                 mx(1, "a", 0)
                 mx(1, "a", 1)
             elif q == 1:
-                evac(7, "s")
+                evac(7, "v")
                 pe_xt(10, "yT0")
                 pe_xt(11, "xt")
                 quant(1)
             elif q == 2:
-                evac(9, "v")
-                evac(11, "s")
-                pe_xt(13)
                 evac(10, "v")
-                quant(2)
+                evac(11, "v")
+                pe_xt(13)
             else:
                 evac(2 * q + 7)
             pe_yt(rows, 2)
@@ -490,6 +507,7 @@ def tile_modelnew_kernel(
             pe_wt(rows)
             s_sq(q, "v", 0)
             s_sq(q, "v", 1)
+            weigh(q - 1, "a", "s", "rest")
             v_cubic(q, "v", 0)
             v_cubic(q, "v", 1)
             if q > 2:
@@ -499,12 +517,18 @@ def tile_modelnew_kernel(
             s_sig(q, "v", 0)
             s_sig(q, "v", 1)
             if q == 0:
-                row_constants()
-                evac(4, "v")
+                row_constants(sums_ps)
+                pe_xt(4, "xt")
+                evac(4, "s")
                 pe_xt(7, "xt")
                 evac(5, "v")
                 pe_xt(8, "w4")
+            elif q == 1:
+                evac(8, "s")
+                pe_xt(12, "w4")
+                evac(9, "v")
             elif q == 2:
+                quant(2)
                 evac(12, "s")
             elif q > 2:
                 evac(2 * q + 8)
@@ -518,8 +542,6 @@ def tile_modelnew_kernel(
         row_red(NQ - 4, "s")
         v_yhat(NQ - 1, 0)
         v_yhat(NQ - 1, 1)
-        weigh(NQ - 1, "v", "s")
-        weigh(NQ - 1, "a")
         scale(NQ - 1, "s")
         spare = ("xt", "a0", "a1", "yT0", "yT1", "v0")
         n = 0
@@ -528,10 +550,40 @@ def tile_modelnew_kernel(
                 if p > NQ - 3 or i >= 2:
                     pe_yt(p, i, spare[n % len(spare)])
                     n += 1
-            pe_wt(p)
+            if p < NQ - 1:
+                pe_wt(p)
             for i in range(4):
                 v_bn(p, i)
-            row_red(p, "s")
+            if p < NQ - 1:
+                row_red(p, "s")
+            if p == NQ - 3:
+                warm = const.tile([P, 1], F32)
+                nc.scalar.activation(out=warm[:], in_=eps1[:], func=ACT.Sqrt, bias=zero[:, 0:1], scale=1.0)
+            if p == NQ - 3:
+                last = c_of[NB - 1]
+                total = work2.tile([P, HW], F32, tag="z", name="total")
+                nc.vector.tensor_scalar(
+                    out=total[:], in0=last[:, 2, HW:BW], scalar1=gw_c[:, 2:3], scalar2=None, op0=ALU.mult
+                )
+                add_weighted = (3,)
+            elif p == NQ - 2:
+                add_weighted = (0, 1)
+            else:
+                add_weighted = ()
+            for j in add_weighted:
+                nc.vector.scalar_tensor_tensor(
+                    out=total[:],
+                    in0=last[:, j, HW:BW],
+                    scalar=gw_c[:, j : j + 1],
+                    in1=total[:],
+                    op0=ALU.mult,
+                    op1=ALU.add,
+                )
+        w4 = psum.tile([P, 4, P], F32, tag="w4", name="w4")
+        for i in range(4):
+            nc.tensor.transpose(w4[:, i, :], total[:, i * P : (i + 1) * P], ident[:])
+        w4_of[NQ - 1] = w4
+        row_red(NQ - 1, "s")
 
         d = const.tile([P, NT], F32)
         vs = const.tile([P, NT], F32)
@@ -544,10 +596,9 @@ def tile_modelnew_kernel(
             out=d[:], in0=d[:], scalar=float(OUT // 4), in1=d[:], op0=ALU.mult, op1=ALU.mult
         )
         nc.vector.tensor_tensor(out=vs[:], in0=vs[:], in1=d[:], op=ALU.add)
-        nc.gpsimd.tensor_tensor(out=vs[:], in0=vs[:], in1=mhalf[:], op=ALU.pow)
-        nc.vector.scalar_tensor_tensor(
-            out=res[:], in0=traw[:], scalar=1.0 / math.sqrt(OUT), in1=vs[:], op0=ALU.mult, op1=ALU.mult
-        )
+        nc.scalar.activation(out=vs[:], in_=vs[:], func=ACT.Sqrt, bias=zero[:, 0:1], scale=float(OUT))
+        nc.vector.reciprocal(out=vs[:], in_=vs[:])
+        nc.vector.tensor_tensor(out=res[:], in0=traw[:], in1=vs[:], op=ALU.mult)
         nc.vector.tensor_scalar(
             out=res[:], in0=res[:], scalar1=mgb[:, 0:1], scalar2=0.0, op0=ALU.add, op1=ALU.max
         )

@@ -26,7 +26,7 @@ NB = NT // BT
 NJ = OUT // P
 NQ = 2 * NB
 XBUFS = 8
-KEEP = 128
+KEEP = 192
 TINY = 1e-18
 
 FLOPS = 2 * B * IN * OUT
@@ -144,6 +144,8 @@ def tile_modelnew_kernel(
         mgb = const.tile([P, 1], F32)
 
         st = const.tile([P, NT, 6], F32)
+        for p in (NQ - 3, NQ - 2):
+            nc.vector.memset(st[:, 4 * p + 3, :], 0.0)
         traw = const.tile([P, NT], F32)
         junk_r = const.tile([P, OUT], F32)
 
@@ -459,12 +461,17 @@ def tile_modelnew_kernel(
                 load_block(s + XBUFS - 1)
             v_yhat(q - 1, 0)
             v_yhat(q - 1, 1)
+            if q == 1:
+                quant(1, 0, HW)
+            if q in (2, 3):
+                quant(2, (q - 2) * HW, HW)
             s_z(q, 0)
             s_sq(q, "a", 0)
             s_z(q, 1)
             s_sq(q, "a", 1)
-            weigh(q - 1, "v")
-            weigh(q - 1, "a", "g", "most")
+            if q < NQ - 1:
+                weigh(q - 1, "v")
+                weigh(q - 1, "a", "g", "most")
             scale(q - 1)
             if q > 0:
                 mx(q, "v", 0)
@@ -490,7 +497,7 @@ def tile_modelnew_kernel(
                 evac(7, "v")
                 pe_xt(10, "yT0")
                 pe_xt(11, "xt")
-                quant(1)
+                quant(1, HW, HW)
             elif q == 2:
                 evac(10, "v")
                 evac(11, "v")
@@ -507,7 +514,8 @@ def tile_modelnew_kernel(
             pe_wt(rows)
             s_sq(q, "v", 0)
             s_sq(q, "v", 1)
-            weigh(q - 1, "a", "s", "rest")
+            if q < NQ - 1:
+                weigh(q - 1, "a", "s", "rest")
             v_cubic(q, "v", 0)
             v_cubic(q, "v", 1)
             if q > 2:
@@ -528,7 +536,6 @@ def tile_modelnew_kernel(
                 pe_xt(12, "w4")
                 evac(9, "v")
             elif q == 2:
-                quant(2)
                 evac(12, "s")
             elif q > 2:
                 evac(2 * q + 8)
@@ -539,51 +546,77 @@ def tile_modelnew_kernel(
             if q > 2:
                 pe_xt(2 * q + 9)
 
+        def s_bn(p, i):
+            t = 4 * p + i
+            nc.scalar.activation(
+                out=junk_r[:], in_=yT_of[(p, i)][:], func=ACT.Copy, scale=-1.0 / OUT, accum_out=negm[:, i : i + 1]
+            )
+            nc.scalar.activation(
+                out=junk_r[:],
+                in_=yT_of[(p, i)][:],
+                func=ACT.Square,
+                bias=negm[:, i : i + 1],
+                scale=1.0,
+                accum_out=st[:, t, 2:3],
+            )
+
+        last = c_of[NB - 1]
+        total = const.tile([P, BW], F32)
+
+        def add_weighted(h, j, first):
+            cols = slice(h * HW, (h + 1) * HW)
+            if first:
+                nc.vector.tensor_scalar(
+                    out=total[:, cols], in0=last[:, j, cols], scalar1=gw_c[:, j : j + 1], scalar2=None, op0=ALU.mult
+                )
+            else:
+                nc.vector.scalar_tensor_tensor(
+                    out=total[:, cols],
+                    in0=last[:, j, cols],
+                    scalar=gw_c[:, j : j + 1],
+                    in1=total[:, cols],
+                    op0=ALU.mult,
+                    op1=ALU.add,
+                )
+
         row_red(NQ - 4, "s")
         v_yhat(NQ - 1, 0)
         v_yhat(NQ - 1, 1)
         scale(NQ - 1, "s")
-        spare = ("xt", "a0", "a1", "yT0", "yT1", "v0")
+        spare = ("xt", "a0", "a1", "v0", "v1", "yT0", "yT1")
+        tiles = [(NQ - 3, 2), (NQ - 3, 3)] + [(p, i) for p in (NQ - 2, NQ - 1) for i in range(4)]
         n = 0
+
+        def fill(upto):
+            for k in range(n, upto):
+                pe_yt(tiles[k][0], tiles[k][1], spare[k % len(spare)])
+            return upto
+
         for p in range(NQ - 3, NQ):
-            for i in range(4):
-                if p > NQ - 3 or i >= 2:
-                    pe_yt(p, i, spare[n % len(spare)])
-                    n += 1
-            if p < NQ - 1:
+            h = p - (NQ - 3)
+            if p == NQ - 3:
+                n = fill(5)
                 pe_wt(p)
+            order = ((2, True), (3, False), (0, False), (1, False))
             for i in range(4):
-                v_bn(p, i)
-            if p < NQ - 1:
-                row_red(p, "s")
+                if h < 2:
+                    add_weighted(h, order[i][0], order[i][1])
+                if i < 3 or p == NQ - 1:
+                    v_bn(p, i)
+                else:
+                    negm = const.tile([P, 4], F32, tag="negm%d" % p, name="negm")
+                    s_bn(p, i)
+            n = fill(min(n + 4, len(tiles)))
+            row_red(p, "s")
+            if h < 2:
+                w4 = psum.tile([P, 4, P], F32, tag="w4", name="w4")
+                for i in range(4):
+                    c0 = h * HW + i * P
+                    nc.tensor.transpose(w4[:, i, :], total[:, c0 : c0 + P], ident[:])
+                w4_of[p + 1] = w4
             if p == NQ - 3:
                 warm = const.tile([P, 1], F32)
                 nc.scalar.activation(out=warm[:], in_=eps1[:], func=ACT.Sqrt, bias=zero[:, 0:1], scale=1.0)
-            if p == NQ - 3:
-                last = c_of[NB - 1]
-                total = work2.tile([P, HW], F32, tag="z", name="total")
-                nc.vector.tensor_scalar(
-                    out=total[:], in0=last[:, 2, HW:BW], scalar1=gw_c[:, 2:3], scalar2=None, op0=ALU.mult
-                )
-                add_weighted = (3,)
-            elif p == NQ - 2:
-                add_weighted = (0, 1)
-            else:
-                add_weighted = ()
-            for j in add_weighted:
-                nc.vector.scalar_tensor_tensor(
-                    out=total[:],
-                    in0=last[:, j, HW:BW],
-                    scalar=gw_c[:, j : j + 1],
-                    in1=total[:],
-                    op0=ALU.mult,
-                    op1=ALU.add,
-                )
-        w4 = psum.tile([P, 4, P], F32, tag="w4", name="w4")
-        for i in range(4):
-            nc.tensor.transpose(w4[:, i, :], total[:, i * P : (i + 1) * P], ident[:])
-        w4_of[NQ - 1] = w4
-        row_red(NQ - 1, "s")
 
         d = const.tile([P, NT], F32)
         vs = const.tile([P, NT], F32)

@@ -26,7 +26,7 @@ NB = NT // BT
 NJ = OUT // P
 NQ = 2 * NB
 XBUFS = 8
-KEEP = 192
+KEEP = 128
 TINY = 1e-18
 
 FLOPS = 2 * B * IN * OUT
@@ -518,8 +518,6 @@ def tile_modelnew_kernel(
                 weigh(q - 1, "a", "s", "rest")
             v_cubic(q, "v", 0)
             v_cubic(q, "v", 1)
-            if q > 2:
-                quant((q + 3) // 2, (q + 3) % 2 * HW, HW)
             s_sig(q, "a")
             g_mul(q)
             s_sig(q, "v", 0)
@@ -540,6 +538,8 @@ def tile_modelnew_kernel(
             elif q > 2:
                 evac(2 * q + 8)
             v_bn(rows, 2)
+            if q > 2:
+                quant((q + 3) // 2, (q + 3) % 2 * HW, HW)
             v_bn(rows, 3)
             pe_yt(rows + 1, 0)
             pe_yt(rows + 1, 1)

import math
from contextlib import ExitStack

import concourse.mybir as mybir
from concourse.masks import make_identity

F32 = mybir.dt.float32
BF16 = mybir.dt.bfloat16
U32 = mybir.dt.uint32
U8 = mybir.dt.uint8
FP8X4 = mybir.dt.float8_e4m3fn_x4
ACT = mybir.ActivationFunctionType
ALU = mybir.AluOpType
AX = mybir.AxisListType

P = 128
B, IN, OUT = 16384, 512, 512
EPS = 1e-5
C1, C2 = 0.797885, 0.035677
NT = B // P
HW = 512
HT = HW // P
BW = 2 * HW
BT = BW // P
NB = NT // BT
NJ = OUT // P
NQ = 2 * NB
XBUFS = 8
KEEP = 128
TINY = 1e-18

FLOPS = 2 * B * IN * OUT


def tile_modelnew_kernel(
    tc, x, weight, bias, bn_weight, bn_bias, bn_mean, bn_var, gn_weight, gn_bias, out
):
    nc = tc.nc
    with ExitStack() as ctx:
        ctx.enter_context(tc.manual_schedule())
        const = ctx.enter_context(tc.tile_pool(name="const", bufs=1))
        xin = ctx.enter_context(tc.tile_pool(name="xin", bufs=XBUFS))
        work2 = ctx.enter_context(tc.tile_pool(name="work2", bufs=2))
        work3 = ctx.enter_context(tc.tile_pool(name="work3", bufs=3))
        psum = ctx.enter_context(tc.psum_pool(name="psum", bufs=1))

        w_sb = [const.tile([P, 2 * IN], BF16, tag="w_sb%d" % i, name="w_sb") for i in range(2)]

        def load_weights(i):
            nc.sync.dma_start(
                out=w_sb[i][:].rearrange("p (j k) -> p j k", k=IN),
                in_=weight[2 * i * P : 2 * (i + 1) * P, :].rearrange("(j p) k -> p j k", p=P),
            )

        load_weights(0)
        zero = const.tile([P, 1], F32)
        nc.vector.memset(zero[:], 0.0)
        warm0 = const.tile([P, 1], F32)
        nc.scalar.activation(out=warm0[:], in_=zero[:], func=ACT.Sigmoid, bias=zero[:, 0:1], scale=1.0)

        pv = const.tile([P, P], BF16)
        nc.gpsimd.memset(pv[:], 0.0)
        for v, vec in enumerate((bias, bn_weight, bn_bias, bn_mean, bn_var)):
            nc.scalar.dma_start(
                out=pv[NJ * v : NJ * v + NJ, :], in_=vec.rearrange("(j p) -> j p", p=P)
            )
        pv2 = const.tile([P, P], BF16)
        nc.gpsimd.memset(pv2[:], 0.0)
        mhalf = const.tile([P, NJ], F32)
        nc.vector.memset(mhalf[:], -0.5)
        ones = const.tile([P, P], F32)
        nc.gpsimd.memset(ones[:], 1.0)
        eps1 = const.tile([P, 1], F32)
        nc.vector.memset(eps1[:], 1.0)

        x_rows = x.rearrange("(p t) k -> p (t k)", t=NT)
        x_of = {}

        def load_block(s):
            if s < NB:
                xc = xin.tile([P, BT * IN], BF16, tag="x", name="xc")
                n = HT * IN if s == 0 else BT * IN
                for c0 in range(0, BT * IN, n):
                    nc.sync.dma_start(
                        out=xc[:, c0 : c0 + n],
                        in_=x_rows[:, s * BT * IN + c0 : s * BT * IN + c0 + n],
                    )
                    if s == 0 and c0 == 0:
                        load_weights(1)
                x_of[s] = xc
            if s == 0:
                for v, vec in enumerate((gn_weight, gn_bias)):
                    nc.sync.dma_start(
                        out=pv2[NJ * v : NJ * v + NJ, :], in_=vec.rearrange("(j p) -> j p", p=P)
                    )

        for s in range(XBUFS):
            load_block(s)

        ident = const.tile([P, P], F32)
        make_identity(nc, ident[:])
        ident_b = const.tile([P, P], BF16)
        make_identity(nc, ident_b[:])

        def transposes(src, col0, b, tag):
            words = src[:].bitcast(F32)
            xt = psum.tile([P, 2, 2, P], F32, tag=tag, name="xt_" + tag)
            for t2 in range(2):
                for u in range(2):
                    w0 = col0 // 2 + (2 * b + t2) * (IN // 2)
                    nc.tensor.transpose(
                        xt[:, t2, u, :], words[:, w0 + u : w0 + IN // 2 : 2], ident[:]
                    )
            return xt

        def copy_out(grouped, xt, b, engine):
            gw32 = grouped[:].bitcast(F32)
            dst = gw32[:, b * 512 : (b + 1) * 512].rearrange("p (t r u) -> p t r u", t=2, u=2)
            srcv = xt[:].rearrange("p t u r -> p t r u")
            if engine == "s":
                nc.scalar.copy(out=dst, in_=srcv)
            else:
                nc.vector.tensor_copy(out=dst, in_=srcv)

        wq = const.tile([P, OUT], U32, align_bytes=64)
        ws = const.tile([P, OUT], U8, align_bytes=64)
        pf = const.tile([P, 5 * NJ], F32)
        gf = const.tile([P, 2 * NJ], F32)
        a_c = const.tile([P, NJ], F32)
        b_c = const.tile([P, NJ], F32)
        d_c = const.tile([P, NJ], F32)
        be_c = const.tile([P, NJ], F32)
        wa_c = const.tile([P, NJ], F32)
        tmp = const.tile([P, NJ], F32)
        r = math.sqrt(C2)
        sc1 = const.tile([P, NJ], F32)
        bi1 = const.tile([P, NJ], F32)
        s_c = const.tile([P, NJ], F32)
        sc2 = const.tile([P, NJ], F32)
        bi2 = const.tile([P, NJ], F32)
        bb = const.tile([P, NJ], F32)
        sums = const.tile([P, 2], F32)
        gw_c = const.tile([P, NJ], F32)
        mgb = const.tile([P, 1], F32)

        st = const.tile([P, NT, 6], F32)
        for p in (NQ - 3, NQ - 2):
            nc.vector.memset(st[:, 4 * p + 3, :], 0.0)
        traw = const.tile([P, NT], F32)
        junk_r = const.tile([P, OUT], F32)

        banks_of = {}
        grouped_of = {}
        xq_of = {}
        acc_of = {}
        c_of = {}
        z_of = {}
        w_of = {}
        w4_of = {}
        yT_of = {}

        def okb(s):
            return 0 <= s < NB

        def okq(q):
            return 0 <= q < NQ

        def units(q, kind):
            if not okq(q):
                return []
            j0 = 0 if kind == "a" else 2
            if q // 2 in (0, NB - 1):
                return [(j0, q % 2), (j0 + 1, q % 2)]
            return [(j0 + q % 2, 0), (j0 + q % 2, 1)]

        def runs(q, kind):
            us = units(q, kind)
            if us and us[0][0] == us[1][0]:
                return [(us[0][0], 0, BW)]
            return [(j, h * HW, HW) for j, h in us]

        def c_at(q, j, c0, n):
            return c_of[q // 2][:, j, c0 : c0 + n]

        def pe_xt(n, tag="xt"):
            if okb(n // 4):
                banks_of[n] = transposes(x_of[n // 4], (n % 4) * 2 * IN, 0, tag)

        def evac(n, engine="s"):
            if okb(n // 4):
                if n % 4 == 0:
                    grouped_of[n // 4] = work2.tile(
                        [P, BW * 4], BF16, tag="grouped", name="grouped", align_bytes=64
                    )
                copy_out(grouped_of[n // 4], banks_of[n], n % 4, engine)

        def quant(s, c0=0, n=BW):
            if okb(s):
                if c0 == 0:
                    xq = work2.tile([P, BW], U32, tag="xq", align_bytes=64)
                    xs = work2.tile([P, BW], U8, tag="xs", align_bytes=64)
                    xq_of[s] = (xq, xs)
                xq, xs = xq_of[s]
                nc.vector.quantize_mx(
                    out=xq[:, c0 : c0 + n].bitcast(FP8X4),
                    scales=xs[:, c0 : c0 + n],
                    in_=grouped_of[s][:, 4 * c0 : 4 * (c0 + n)],
                )

        def mx(q, kind, i):
            for j, h in units(q, kind)[i : i + 1]:
                xq, xs = xq_of[q // 2]
                tag = "%s%d" % (kind, i)
                acc = psum.tile([P, HW], F32, tag=tag, name="acc_" + tag)
                cols = slice(h * HW, (h + 1) * HW)
                nc.tensor.matmul_mx(
                    out=acc[:],
                    lhsT=wq[:, j * P : (j + 1) * P].bitcast(FP8X4),
                    lhsT_scale=ws[:, j * P : (j + 1) * P],
                    rhs=xq[:, cols].bitcast(FP8X4),
                    rhs_scale=xs[:, cols],
                    start=True,
                    stop=True,
                )
                acc_of[(q, kind, i)] = acc

        def s_z(q, i):
            for j, h in units(q, "a")[i : i + 1]:
                if i == 0:
                    z_of[q] = work2.tile([P, BW], F32, tag="z", name="z")
                nc.scalar.activation(
                    out=z_of[q][:, i * HW : (i + 1) * HW],
                    in_=acc_of[(q, "a", i)][:],
                    func=ACT.Identity,
                    bias=b_c[:, j : j + 1],
                    scale=a_c[:, j : j + 1],
                )

        def s_sq(q, kind, i):
            for j, h in units(q, kind)[i : i + 1]:
                if q // 2 not in c_of:
                    c_of[q // 2] = work3.tile([P, NJ, BW], F32, tag="c", name="c")
                nc.scalar.activation(
                    out=c_at(q, j, h * HW, HW),
                    in_=acc_of[(q, kind, i)][:],
                    func=ACT.Square,
                    bias=bi1[:, j : j + 1],
                    scale=sc1[:, j : j + 1],
                )

        def v_cubic(q, kind, i):
            for j, h in units(q, kind)[i : i + 1]:
                cj = c_at(q, j, h * HW, HW)
                nc.vector.scalar_tensor_tensor(
                    out=cj,
                    in0=cj,
                    scalar=s_c[:, j : j + 1],
                    in1=acc_of[(q, kind, i)][:],
                    op0=ALU.add,
                    op1=ALU.mult,
                )

        def s_sig(q, kind, i=None):
            parts = runs(q, kind) if i is None else [(j, h * HW, HW) for j, h in units(q, kind)[i : i + 1]]
            for j, c0, n in parts:
                cj = c_at(q, j, c0, n)
                nc.scalar.activation(
                    out=cj,
                    in_=cj,
                    func=ACT.Sigmoid,
                    bias=bi2[:, j : j + 1],
                    scale=sc2[:, j : j + 1],
                )

        def v_yhat(q, i):
            for j, h in units(q, "v")[i : i + 1]:
                cj = c_at(q, j, h * HW, HW)
                nc.vector.scalar_tensor_tensor(
                    out=cj,
                    in0=acc_of[(q, "v", i)][:],
                    scalar=be_c[:, j : j + 1],
                    in1=cj,
                    op0=ALU.add,
                    op1=ALU.mult,
                )

        def g_mul(q):
            z0 = 0
            for j, c0, n in runs(q, "a"):
                cj = c_at(q, j, c0, n)
                nc.gpsimd.tensor_tensor(out=cj, in0=cj, in1=z_of[q][:, z0 : z0 + n], op=ALU.mult)
                z0 += n

        def product(dst, src, factor, engine):
            if engine == "g":
                nc.gpsimd.tensor_scalar(
                    out=dst, in0=src, scalar1=factor, scalar2=zero[:, 0:1], op0=ALU.mult, op1=ALU.add
                )
            else:
                nc.scalar.activation(out=dst, in_=src, func=ACT.Copy, scale=factor)

        def weigh(q, kind, engine="g", part=None):
            for j, c0, n in runs(q, kind):
                s = q // 2
                if part == "most":
                    n -= KEEP
                elif part == "rest":
                    c0, n = c0 + n - KEEP, KEEP
                if s not in w_of:
                    w_of[s] = work2.tile([P, NJ, BW], F32, tag="w", name="w")
                factor = gw_c[:, j : j + 1] if kind == "a" else wa_c[:, j : j + 1]
                product(w_of[s][:, j, c0 : c0 + n], c_at(q, j, c0, n), factor, engine)

        def scale(q, engine="g"):
            for j, c0, n in runs(q, "v"):
                product(c_at(q, j, c0, n), c_at(q, j, c0, n), d_c[:, j : j + 1], engine)

        def pe_wt(p):
            if okq(p):
                w4 = psum.tile([P, 4, P], F32, tag="w4", name="w4")
                for i in range(4):
                    t = 4 * (p % 2) + i
                    for j in range(NJ):
                        nc.tensor.matmul(
                            out=w4[:, i, :],
                            lhsT=w_of[p // 2][:, j, t * P : (t + 1) * P],
                            rhs=ident[:],
                            is_transpose=True,
                            start=(j == 0),
                            stop=(j == NJ - 1),
                        )
                w4_of[p] = w4

        def row_red(p, engine="v"):
            if okq(p) and engine == "s":
                for i in range(4):
                    nc.scalar.activation(
                        out=junk_r[:, i * P : (i + 1) * P],
                        in_=w4_of[p][:, i, :],
                        func=ACT.Copy,
                        accum_out=traw[:, 4 * p + i : 4 * p + i + 1],
                    )
            elif okq(p):
                nc.vector.tensor_reduce(
                    out=traw[:, 4 * p : 4 * p + 4], in_=w4_of[p][:], axis=AX.X, op=ALU.add
                )

        def pe_yt(p, i, tag=None):
            if okq(p):
                tag = tag or "yT%d" % (i % 2)
                yT = psum.tile([P, OUT], F32, tag=tag, name="yT_" + tag)
                t = 4 * (p % 2) + i
                for j in range(NJ):
                    nc.tensor.transpose(
                        yT[:, j * P : (j + 1) * P], c_of[p // 2][:, j, t * P : (t + 1) * P], ident[:]
                    )
                yT_of[(p, i)] = yT

        def v_bn(p, i):
            if okq(p):
                nc.vector.bn_stats(out=st[:, 4 * p + i, :], in_=yT_of[(p, i)][:])

        w_grouped = const.tile([P, OUT * 4], BF16, align_bytes=64)
        blank = const.tile([P, HW], BF16)
        nc.vector.memset(blank[:], 0.0)

        def warm_up(n, tag):
            blank_ps = psum.tile([P, HW], F32, tag=tag, name="blank_ps")
            for i in range(n):
                nc.tensor.matmul(
                    out=blank_ps[:], lhsT=blank[:, 0:P], rhs=blank[:], start=True, stop=True
                )

        warm_up(4, "w4")
        w_bank0 = transposes(w_sb[0], 0, 0, "a0")
        pe_xt(0, "v0")
        pT = psum.tile([P, P], BF16, tag="yT0", name="pT")
        nc.tensor.transpose(pT[:], pv[:], ident_b[:])
        pe_xt(1, "v1")
        w_bank1 = transposes(w_sb[1], 0, 0, "a1")

        def quant_w(i):
            cols = slice(2 * i * P, 2 * (i + 1) * P)
            nc.vector.quantize_mx(
                out=wq[:, cols].bitcast(FP8X4),
                scales=ws[:, cols],
                in_=w_grouped[:, 4 * cols.start : 4 * cols.stop],
            )

        copy_out(w_grouped, w_bank0, 0, "v")
        evac(0, "s")
        evac(1, "s")
        quant_w(0)
        nc.vector.tensor_copy(out=pf[:], in_=pT[:, 0 : 5 * NJ])
        nc.vector.tensor_scalar(
            out=a_c[:], in0=pf[:, 4 * NJ : 5 * NJ], scalar1=EPS, scalar2=None, op0=ALU.add
        )
        nc.gpsimd.tensor_tensor(out=a_c[:], in0=a_c[:], in1=mhalf[:], op=ALU.pow)
        nc.vector.tensor_tensor(
            out=b_c[:], in0=pf[:, 0:NJ], in1=pf[:, 3 * NJ : 4 * NJ], op=ALU.subtract
        )
        copy_out(w_grouped, w_bank1, 1, "s")
        quant(0, 0, HW)
        nc.vector.tensor_tensor(out=a_c[:], in0=a_c[:], in1=pf[:, NJ : 2 * NJ], op=ALU.mult)
        pe_xt(2, "w4")
        evac(2, "s")
        mx(0, "a", 0)
        mx(0, "a", 1)
        nc.vector.tensor_tensor(out=b_c[:], in0=b_c[:], in1=a_c[:], op=ALU.mult)
        nc.vector.tensor_scalar(out=sc1[:], in0=a_c[:], scalar1=r, scalar2=None, op0=ALU.mult)
        quant_w(1)
        nc.vector.tensor_tensor(out=b_c[:], in0=b_c[:], in1=pf[:, 2 * NJ : 3 * NJ], op=ALU.add)
        nc.vector.tensor_scalar(out=sc2[:], in0=a_c[:], scalar1=2.0, scalar2=None, op0=ALU.mult)
        nc.vector.tensor_scalar(out=bi1[:], in0=b_c[:], scalar1=1.5 * r, scalar2=None, op0=ALU.mult)
        nc.vector.tensor_tensor(out=bb[:], in0=b_c[:], in1=b_c[:], op=ALU.mult)
        nc.vector.tensor_scalar(
            out=s_c[:], in0=bb[:], scalar1=0.75 * C2, scalar2=C1, op0=ALU.mult, op1=ALU.add
        )
        nc.vector.tensor_scalar(
            out=bb[:], in0=bb[:], scalar1=2.0 * C2, scalar2=2.0 * C1, op0=ALU.mult, op1=ALU.add
        )
        nc.vector.tensor_tensor(out=bi2[:], in0=bb[:], in1=b_c[:], op=ALU.mult)
        nc.gpsimd.tensor_tensor(out=tmp[:], in0=a_c[:], in1=a_c[:], op=ALU.mult)
        nc.gpsimd.tensor_scalar(
            out=tmp[:], in0=tmp[:], scalar1=TINY * TINY, scalar2=2.0 * TINY, op0=ALU.is_lt, op1=ALU.mult
        )
        nc.gpsimd.tensor_tensor(out=d_c[:], in0=a_c[:], in1=tmp[:], op=ALU.add)
        nc.vector.reciprocal(out=be_c[:], in_=d_c[:])
        nc.vector.tensor_tensor(out=be_c[:], in0=be_c[:], in1=b_c[:], op=ALU.mult)
        mx(0, "v", 0)
        mx(0, "v", 1)
        pe_xt(3, "yT1")
        gT = psum.tile([P, P], BF16, tag="yT0", name="gT")
        nc.tensor.transpose(gT[:], pv2[:], ident_b[:])

        def row_sums():
            nc.vector.tensor_copy(out=gf[:], in_=gT[:, 0 : 2 * NJ])
            sums_ps = psum.tile([P, 2 * NJ], F32, tag="xt", name="sums_ps")
            nc.tensor.matmul(out=sums_ps[:], lhsT=ones[:], rhs=gf[:], start=True, stop=True)
            return sums_ps

        def row_constants(sums_ps):
            nc.vector.tensor_reduce(
                out=sums[:], in_=sums_ps[:].rearrange("p (v j) -> p v j", v=2), axis=AX.X, op=ALU.add
            )
            nc.vector.tensor_scalar(
                out=mgb[:], in0=sums[:, 1:2], scalar1=1.0 / OUT, scalar2=None, op0=ALU.mult
            )
            nc.vector.tensor_scalar(
                out=sums[:, 0:1], in0=sums[:, 0:1], scalar1=-1.0 / OUT, scalar2=None, op0=ALU.mult
            )
            nc.vector.tensor_scalar(
                out=gw_c[:], in0=gf[:, 0:NJ], scalar1=sums[:, 0:1], scalar2=None, op0=ALU.add
            )
            nc.gpsimd.tensor_tensor(out=wa_c[:], in0=d_c[:], in1=gw_c[:], op=ALU.mult)

        for q in range(NQ):
            s, pp = q // 2, q % 2
            rows = q - 3
            if pp == 0 and s > 0:
                load_block(s + XBUFS - 1)
            v_yhat(q - 1, 0)
            v_yhat(q - 1, 1)
            if q == 1:
                quant(1, 0, HW)
            if q in (2, 3):
                quant(2, (q - 2) * HW, HW)
            s_z(q, 0)
            s_sq(q, "a", 0)
            s_z(q, 1)
            s_sq(q, "a", 1)
            if q < NQ - 1:
                weigh(q - 1, "v")
                weigh(q - 1, "a", "g", "most")
            scale(q - 1)
            if q > 0:
                mx(q, "v", 0)
                mx(q, "v", 1)
            row_red(rows - 1)
            v_bn(rows, 0)
            v_cubic(q, "a", 0)
            v_bn(rows, 1)
            if q == 0:
                pe_xt(5, "w4")
                evac(3, "v")
                pe_xt(6, "yT1")
            elif q == 1:
                evac(6, "s")
                pe_xt(9, "yT1")
            v_cubic(q, "a", 1)
            if q == 0:
                sums_ps = row_sums()
                quant(0, HW, HW)
                mx(1, "a", 0)
                mx(1, "a", 1)
            elif q == 1:
                evac(7, "v")
                pe_xt(10, "yT0")
                pe_xt(11, "xt")
                quant(1, HW, HW)
            elif q == 2:
                evac(10, "v")
                evac(11, "v")
                pe_xt(13)
            else:
                evac(2 * q + 7)
            pe_yt(rows, 2)
            if q > 2:
                pe_xt(2 * q + 8)
            pe_yt(rows, 3)
            if q > 0:
                mx(q + 1, "a", 0)
                mx(q + 1, "a", 1)
            pe_wt(rows)
            s_sq(q, "v", 0)
            s_sq(q, "v", 1)
            if q < NQ - 1:
                weigh(q - 1, "a", "s", "rest")
            v_cubic(q, "v", 0)
            v_cubic(q, "v", 1)
            s_sig(q, "a")
            g_mul(q)
            s_sig(q, "v", 0)
            s_sig(q, "v", 1)
            if q == 0:
                row_constants(sums_ps)
                pe_xt(4, "xt")
                evac(4, "s")
                pe_xt(7, "xt")
                evac(5, "v")
                pe_xt(8, "w4")
            elif q == 1:
                evac(8, "s")
                pe_xt(12, "w4")
                evac(9, "v")
            elif q == 2:
                evac(12, "s")
            elif q > 2:
                evac(2 * q + 8)
            v_bn(rows, 2)
            if q > 2:
                quant((q + 3) // 2, (q + 3) % 2 * HW, HW)
            v_bn(rows, 3)
            pe_yt(rows + 1, 0)
            pe_yt(rows + 1, 1)
            if q > 2:
                pe_xt(2 * q + 9)

        def s_bn(p, i):
            t = 4 * p + i
            nc.scalar.activation(
                out=junk_r[:], in_=yT_of[(p, i)][:], func=ACT.Copy, scale=-1.0 / OUT, accum_out=negm[:, i : i + 1]
            )
            nc.scalar.activation(
                out=junk_r[:],
                in_=yT_of[(p, i)][:],
                func=ACT.Square,
                bias=negm[:, i : i + 1],
                scale=1.0,
                accum_out=st[:, t, 2:3],
            )

        last = c_of[NB - 1]
        total = const.tile([P, BW], F32)

        def add_weighted(h, j, first):
            cols = slice(h * HW, (h + 1) * HW)
            if first:
                nc.vector.tensor_scalar(
                    out=total[:, cols], in0=last[:, j, cols], scalar1=gw_c[:, j : j + 1], scalar2=None, op0=ALU.mult
                )
            else:
                nc.vector.scalar_tensor_tensor(
                    out=total[:, cols],
                    in0=last[:, j, cols],
                    scalar=gw_c[:, j : j + 1],
                    in1=total[:, cols],
                    op0=ALU.mult,
                    op1=ALU.add,
                )

        row_red(NQ - 4, "s")
        v_yhat(NQ - 1, 0)
        v_yhat(NQ - 1, 1)
        scale(NQ - 1, "s")
        spare = ("xt", "a0", "a1", "v0", "v1", "yT0", "yT1")
        tiles = [(NQ - 3, 2), (NQ - 3, 3)] + [(p, i) for p in (NQ - 2, NQ - 1) for i in range(4)]
        n = 0

        def fill(upto):
            for k in range(n, upto):
                pe_yt(tiles[k][0], tiles[k][1], spare[k % len(spare)])
            return upto

        for p in range(NQ - 3, NQ):
            h = p - (NQ - 3)
            if p == NQ - 3:
                n = fill(5)
                pe_wt(p)
            order = ((2, True), (3, False), (0, False), (1, False))
            for i in range(4):
                if h < 2:
                    add_weighted(h, order[i][0], order[i][1])
                if i < 3 or p == NQ - 1:
                    v_bn(p, i)
                else:
                    negm = const.tile([P, 4], F32, tag="negm%d" % p, name="negm")
                    s_bn(p, i)
            n = fill(min(n + 4, len(tiles)))
            row_red(p, "s")
            if h < 2:
                w4 = psum.tile([P, 4, P], F32, tag="w4", name="w4")
                for i in range(4):
                    c0 = h * HW + i * P
                    nc.tensor.transpose(w4[:, i, :], total[:, c0 : c0 + P], ident[:])
                w4_of[p + 1] = w4
            if p == NQ - 3:
                warm = const.tile([P, 1], F32)
                nc.scalar.activation(out=warm[:], in_=eps1[:], func=ACT.Sqrt, bias=zero[:, 0:1], scale=1.0)

        d = const.tile([P, NT], F32)
        vs = const.tile([P, NT], F32)
        res = const.tile([P, NT], F32)
        nc.vector.tensor_tensor(out=d[:], in0=st[:, :, 1], in1=st[:, :, 4], op=ALU.subtract)
        nc.vector.scalar_tensor_tensor(
            out=vs[:], in0=st[:, :, 2], scalar=EPS * OUT, in1=st[:, :, 5], op0=ALU.add, op1=ALU.add
        )
        nc.vector.scalar_tensor_tensor(
            out=d[:], in0=d[:], scalar=float(OUT // 4), in1=d[:], op0=ALU.mult, op1=ALU.mult
        )
        nc.vector.tensor_tensor(out=vs[:], in0=vs[:], in1=d[:], op=ALU.add)
        nc.scalar.activation(out=vs[:], in_=vs[:], func=ACT.Sqrt, bias=zero[:, 0:1], scale=float(OUT))
        nc.vector.reciprocal(out=vs[:], in_=vs[:])
        nc.vector.tensor_tensor(out=res[:], in0=traw[:], in1=vs[:], op=ALU.mult)
        nc.vector.tensor_scalar(
            out=res[:], in0=res[:], scalar1=mgb[:, 0:1], scalar2=0.0, op0=ALU.add, op1=ALU.max
        )
        nc.sync.dma_start(out=out.rearrange("(p t) o -> p (t o)", t=NT), in_=res[:])
